import numpy as np
import ml_dtypes


def mxq(x, axis, fmt="e4m3"):
    dtype, down = {"e4m3": (ml_dtypes.float8_e4m3fn, 7), "e5m2": (ml_dtypes.float8_e5m2, 14)}[fmt]
    v = np.moveaxis(np.asarray(x, np.float32).astype(ml_dtypes.bfloat16).astype(np.float64), axis, -1)
    blocks = v.reshape(v.shape[:-1] + (-1, 32))
    amax = np.abs(blocks).max(-1, keepdims=True)
    byte = np.maximum(np.where(amax > 0, np.frexp(amax)[1] - 1 + 127, 0) - down, 1)
    scale = np.exp2(byte - 127.0)
    codes = (blocks / scale).astype(np.float32).astype(dtype).astype(np.float64)
    return np.moveaxis((codes * scale).reshape(v.shape), -1, axis)


WIDE = False


def mx_kscale(k):
    if not WIDE:
        return np.ones(k)
    levels = np.array([10, -10, 5, -5, 0])
    if k % 512:
        return np.exp2(np.random.permutation(np.resize(levels, k // 32))).repeat(32)
    a = np.empty((k // 512, 16))
    for p in range(k // 512):
        a[p, :8] = np.random.permutation(np.resize(levels, 8))
        for g in range(8):
            far = levels[np.abs(levels - a[p, g]) >= 10]
            a[p, g + 8] = far[np.random.randint(len(far))]
    return np.exp2(a.ravel()).repeat(32)


BF16 = ml_dtypes.bfloat16


def bf(x):
    return np.asarray(x, np.float32).astype(BF16)


def f64(x):
    return np.asarray(x).astype(np.float64)


B, S, IQ, OQ, Q = 4, 256, 512, 512, 4


def setup_inputs():
    s = mx_kscale(IQ)
    sw = 0.5 / np.sqrt(IQ)
    return {"x": bf((np.random.standard_normal((B, S, IQ, Q)) * s[:, None]).reshape(B, S, IQ * Q)),
            "wr": bf(np.random.standard_normal((OQ, IQ)) * sw / s),
            "wi": bf(np.random.standard_normal((OQ, IQ)) * sw / s),
            "wj": bf(np.random.standard_normal((OQ, IQ)) * sw / s),
            "wk": bf(np.random.standard_normal((OQ, IQ)) * sw / s),
            "bias": bf(np.random.standard_normal(OQ * Q) * 0.3)}


def core(x, wr, wi, wj, wk, bias):
    xq = f64(x).reshape(B * S, IQ, Q)
    xr = mxq(xq[:, :, 0], 1, "e4m3")
    xi = mxq(xq[:, :, 1], 1, "e4m3")
    xj = mxq(xq[:, :, 2], 1, "e4m3")
    xk = mxq(xq[:, :, 3], 1, "e4m3")
    qr = mxq(f64(wr), 1, "e4m3")
    qi = mxq(f64(wi), 1, "e4m3")
    qj = mxq(f64(wj), 1, "e4m3")
    qk = mxq(f64(wk), 1, "e4m3")
    Ar = xr @ qr.T
    Br = xi @ qr.T
    Cr = xj @ qr.T
    Dr = xk @ qr.T
    Ai = xr @ qi.T
    Bi = xi @ qi.T
    Aj = xr @ qj.T
    Cj = xj @ qj.T
    Ak = xr @ qk.T
    Dk = xk @ qk.T
    or_ = Ar - Bi - Cj - Dk
    oi_ = Br + Ai + Dk - Cj
    oj_ = Cr - Dk + Aj + Bi
    ok_ = Dr + Cj - Bi + Ak
    out = np.stack([or_, oi_, oj_, ok_], axis=-1).reshape(B, S, Q * OQ)
    return out + f64(bias)[None, None, :]


def e4m3fn_bytes(y):
    return np.clip(np.asarray(y, np.float64), -448.0, 448.0).astype(np.float32).astype(ml_dtypes.float8_e4m3fn).view(np.uint8)


def reference(x, wr, wi, wj, wk, bias):
    out = core(x, wr, wi, wj, wk, bias)
    s = np.max(np.abs(out)) / 448.0
    return out, e4m3fn_bytes(out / s)

@@ -1,0 +1,302 @@
+from contextlib import ExitStack
+
+import concourse.masks as masks
+import concourse.mybir as mybir
+
+FLOPS = 2 * 10 * 1024 * 512 * 512
+
+F32 = mybir.dt.float32
+BF16 = mybir.dt.bfloat16
+U32 = mybir.dt.uint32
+U8 = mybir.dt.uint8
+FP8 = mybir.dt.float8_e4m3fn
+FP8X4 = mybir.dt.float8_e4m3fn_x4
+ALU = mybir.AluOpType
+ACT = mybir.ActivationFunctionType
+AXIS_X = mybir.AxisListType.X
+
+P = 128
+Q = 4
+N_TILES = 8
+O_CHUNKS = 4
+BANK = 512
+WIDTH = 2048
+
+R = 0
+I = 1
+J = 2
+K = 3
+NI = 4
+NJ = 5
+NK = 6
+WINDOWS = ((R, I, J, K), (NI, R, I, NI), (NJ, NJ, R, J), (NK, K, NK, R))
+
+V_HELP_TILES = 0
+V_COLS = 1376
+SG_FROM = 8
+SG_MOD = 2
+SG_LAST = 29
+G_NEG_FROM = 1
+PEND_PER = 2
+ORDER = [("w", 0), ("x", 0), ("x", 1), ("x", 2), ("x", 3), ("w", 1), ("x", 4), ("x", 5), ("x", 6), ("x", 7), ("w", 2), ("w", 3)]
+
+
+def quantize_runs():
+    flat = [b for win in WINDOWS for b in win]
+    runs = []
+    d = 0
+    while d < len(flat):
+        n = 1
+        for cand in (4, 2):
+            if d + cand <= len(flat) and all(flat[d + e] == flat[d] + e for e in range(cand)):
+                n = cand
+                break
+        runs.append((flat[d], n, d))
+        d += n
+    return runs
+
+
+def tile_quaternionlinear_pa_kernel(tc, x, wr, wi, wj, wk, bias, out_0, out_1):
+    nc = tc.nc
+    xf = x.flatten_outer_dims()
+    o0 = out_0.flatten_outer_dims()
+    o1 = out_1.flatten_outer_dims()
+    weights = (wr, wi, wj, wk)
+
+    with ExitStack() as ctx:
+        const = ctx.enter_context(tc.tile_pool(name="const", bufs=1))
+        keep = ctx.enter_context(tc.tile_pool(name="keep", bufs=1))
+        psum = ctx.enter_context(tc.psum_pool(name="psum", bufs=8))
+        ctx.enter_context(tc.manual_schedule())
+
+        ident_f = const.tile([P, P], F32, name="ident_f")
+        ident_b = const.tile([P, P], BF16, name="ident_b")
+        ones = const.tile([P, P], BF16, name="ones")
+        bias_row = const.tile([P, WIDTH], BF16, name="bias_row")
+        bias_sb = const.tile([P, WIDTH], BF16, name="bias_sb")
+        stats = const.tile([P, N_TILES * O_CHUNKS], F32, name="stats")
+        small = const.tile([P, 8], F32, name="small")
+
+        x_codes = [keep.tile([P, Q * P], U32, name="xc%d" % t, align_bytes=64) for t in range(N_TILES)]
+        x_scales = [keep.tile([P, Q * P], U8, name="xs%d" % t, align_bytes=64) for t in range(N_TILES)]
+        w_codes = [keep.tile([P, Q * BANK], U32, name="wc%d" % c, align_bytes=64) for c in range(O_CHUNKS)]
+        w_scales = [keep.tile([P, Q * BANK], U8, name="ws%d" % c, align_bytes=64) for c in range(O_CHUNKS)]
+        o_sb = [keep.tile([P, WIDTH], F32, name="o%d" % t) for t in range(N_TILES)]
+
+        with ExitStack() as phase1:
+            raw = phase1.enter_context(tc.tile_pool(name="raw", bufs=1))
+            stage = phase1.enter_context(tc.tile_pool(name="stage", bufs=3))
+
+            x_raw = [raw.tile([P, WIDTH], BF16, name="xr%d" % t) for t in range(N_TILES)]
+            w_raw = [raw.tile([P, Q, 512], BF16, name="wr%d" % c) for c in range(O_CHUNKS)]
+
+            nc.vector.memset(bias_row[:], 0.0)
+            nc.vector.memset(ones[:], 1.0)
+            nc.vector.memset(small[:], 1.0)
+            nc.scalar.dma_start(out=bias_row[0:1, :], in_=bias.rearrange("(a n) -> a n", a=1))
+            nc.scalar.activation(out=small[:, 1:2], in_=small[:, 0:1], func=ACT.Copy)
+            masks.make_identity(nc, ident_f[:])
+            masks.make_identity(nc, ident_b[:])
+
+            def load_w(c):
+                for y in range(Q):
+                    nc.sync.dma_start(out=w_raw[c][:, y, :], in_=weights[y][c * P : (c + 1) * P, :])
+
+            def load_x(t):
+                nc.sync.dma_start(out=x_raw[t][:], in_=xf[t * P : (t + 1) * P, :])
+
+            order = ORDER
+            for kind, n in order:
+                if kind == "w":
+                    load_w(n)
+                else:
+                    load_x(n)
+
+            def spread_bias():
+                for h in range(2):
+                    bp = psum.tile([P, 2 * BANK], BF16, name="bank")
+                    for e in range(2):
+                        cols = slice((2 * h + e) * BANK, (2 * h + e + 1) * BANK)
+                        nc.tensor.matmul(out=bp[:, e * BANK : (e + 1) * BANK], lhsT=ones[:], rhs=bias_row[:, cols], start=True, stop=True)
+                    nc.vector.tensor_copy(out=bias_sb[:, 2 * h * BANK : 2 * (h + 1) * BANK], in_=bp[:])
+
+            banks_t = {}
+            grouped = {}
+
+            def transposes(kind, n):
+                pts = []
+                for h in range(2):
+                    if kind == "w":
+                        pt = psum.tile([P, 2, 2, P], F32, name="bank")
+                        for yy in range(2):
+                            words = w_raw[n][:, 2 * h + yy, :].bitcast(F32)
+                            for u in range(2):
+                                nc.tensor.transpose(pt[:, yy, u, :], words[:, u::2], ident_f[:])
+                    else:
+                        pt = psum.tile([P, 8, P], BF16, name="bank")
+                        for cc in range(2):
+                            for t in range(4):
+                                nc.tensor.transpose(pt[:, cc * 4 + t, :], x_raw[n][:, 4 * t + 2 * h + cc :: 16], ident_b[:])
+                    pts.append(pt)
+                banks_t[(kind, n)] = pts
+
+            def empty(kind, n):
+                pts = banks_t[(kind, n)]
+                if kind == "w":
+                    wg = stage.tile([P, 7, 512], BF16, name="wg", bufs=2, align_bytes=64)
+                    for h in range(2):
+                        nc.scalar.copy(
+                            out=wg[:, 2 * h : 2 * h + 2, :].bitcast(F32).rearrange("p y (o u) -> p y o u", u=2),
+                            in_=pts[h][:].rearrange("p y u o -> p y o u"),
+                        )
+                    if n >= G_NEG_FROM:
+                        nc.gpsimd.tensor_scalar(out=wg[:, NI : NK + 1, :], in0=wg[:, I : K + 1, :], scalar1=-1.0, scalar2=0.0, op0=ALU.mult, op1=ALU.add)
+                    grouped[(kind, n)] = wg
+                else:
+                    xg = stage.tile([P, Q, P, 4], BF16, name="xg", bufs=3, align_bytes=64)
+                    for h in range(2):
+                        src = pts[h][:].rearrange("p (c t) n -> p c n t", c=2)
+                        if h == 1 and n < V_HELP_TILES:
+                            nc.vector.tensor_copy(out=xg[:, 2 * h : 2 * h + 2, :, :], in_=src)
+                        else:
+                            nc.scalar.copy(out=xg[:, 2 * h : 2 * h + 2, :, :], in_=src)
+                    grouped[(kind, n)] = xg
+
+            def quantize_steps(kind, n):
+                g = grouped[(kind, n)]
+                steps = []
+                if kind == "x":
+                    steps.append(
+                        lambda: nc.vector.quantize_mx(
+                            out=x_codes[n][:].bitcast(FP8X4), scales=x_scales[n][:], in_=g[:].rearrange("p c n t -> p (c n t)")
+                        )
+                    )
+                    return steps
+                if n < G_NEG_FROM:
+                    steps.append(lambda: nc.vector.tensor_scalar(out=g[:, NI : NK + 1, :], in0=g[:, I : K + 1, :], scalar1=-1.0, scalar2=None, op0=ALU.mult))
+
+                def one(s, cnt, d):
+                    return lambda: nc.vector.quantize_mx(
+                        out=w_codes[n][:, d * P : (d + cnt) * P].bitcast(FP8X4),
+                        scales=w_scales[n][:, d * P : (d + cnt) * P],
+                        in_=g[:, s : s + cnt, :].rearrange("p b e -> p (b e)"),
+                    )
+
+                for s, cnt, d in quantize_runs():
+                    steps.append(one(s, cnt, d))
+                return steps
+
+            all_banks = [(c, t) for c in range(O_CHUNKS) for t in range(N_TILES)]
+            n_banks = len(all_banks)
+            acc_of = {}
+            due = {}
+
+            def by_scalar_and_gpsimd(i):
+                return SG_FROM <= i <= SG_LAST and i % SG_MOD == 0
+
+            def multiply(i):
+                c, t = all_banks[i]
+                acc = psum.tile([P, BANK], F32, name="bank")
+                for comp in range(Q):
+                    nc.tensor.matmul_mx(
+                        out=acc[:],
+                        lhsT=x_codes[t][:, comp * P : (comp + 1) * P].bitcast(FP8X4),
+                        lhsT_scale=x_scales[t][:, comp * P : (comp + 1) * P],
+                        rhs=w_codes[c][:, comp * BANK : (comp + 1) * BANK].bitcast(FP8X4),
+                        rhs_scale=w_scales[c][:, comp * BANK : (comp + 1) * BANK],
+                        start=(comp == 0),
+                        stop=(comp == Q - 1),
+                    )
+                acc_of[i] = acc
+
+            def add_bias(i):
+                c, t = all_banks[i]
+                cols = slice(c * BANK, (c + 1) * BANK)
+                sums = acc_of[i][:].rearrange("p (c o) -> p o c", c=Q)
+                if by_scalar_and_gpsimd(i):
+                    plain = stage.tile([P, BANK], F32, name="plain", bufs=3)
+                    nc.scalar.copy(out=plain[:].rearrange("p (o c) -> p o c", c=Q), in_=sums)
+                    nc.gpsimd.tensor_tensor(out=o_sb[t][:, cols], in0=plain[:], in1=bias_sb[:, cols], op=ALU.add)
+                else:
+                    nc.vector.tensor_tensor(
+                        out=o_sb[t][:, cols].rearrange("p (o c) -> p o c", c=Q),
+                        in0=sums,
+                        in1=bias_sb[:, cols].rearrange("p (o c) -> p o c", c=Q),
+                        op=ALU.add,
+                    )
+                nc.sync.dma_start(out=o0[t * P : (t + 1) * P, cols], in_=o_sb[t][:, cols])
+
+            def abs_max(i):
+                c, t = all_banks[i]
+                nc.vector.tensor_reduce(
+                    out=stats[:, i : i + 1], in_=o_sb[t][:, c * BANK : (c + 1) * BANK], axis=AXIS_X, op=ALU.max, apply_absolute_value=True
+                )
+
+            def bank_step(i):
+                if i < n_banks:
+                    multiply(i)
+                if 1 <= i <= n_banks:
+                    add_bias(i - 1)
+                    lag = 3 if by_scalar_and_gpsimd(i - 1) else 1
+                    due.setdefault(i + lag, []).append(i - 1)
+                for b in due.get(i, []):
+                    abs_max(b)
+
+            transposes(*order[0])
+            transposes(*order[1])
+            pending = []
+            issued = 0
+            done = 0
+            for j in range(len(order)):
+                kind, n = order[j]
+                empty(kind, n)
+                if j == 1:
+                    spread_bias()
+                if j + 2 < len(order):
+                    transposes(*order[j + 2])
+                if kind == "w" and n >= 2:
+                    pending.extend(quantize_steps(kind, n))
+                else:
+                    for step in quantize_steps(kind, n):
+                        step()
+                if kind == "x":
+                    bank_step(done)
+                    done += 1
+            while done < n_banks + 5:
+                bank_step(done)
+                done += 1
+                for step in pending[issued : issued + PEND_PER]:
+                    step()
+                issued += PEND_PER
+
+        nc.vector.tensor_reduce(out=small[:, 2:3], in_=stats[:], axis=AXIS_X, op=ALU.max)
+        spread = psum.tile([P, P], F32, name="bank")
+        nc.tensor.transpose(spread[:], small[:, 2:3].to_broadcast([P, P]), ident_f[:])
+        nc.vector.tensor_reduce(out=small[:, 3:4], in_=spread[:], axis=AXIS_X, op=ALU.max)
+        inverse = small[:, 4:5]
+        nc.vector.reciprocal(out=inverse, in_=small[:, 3:4])
+
+        with ExitStack() as phase2:
+            ypool = phase2.enter_context(tc.tile_pool(name="ypool", bufs=3))
+            qpool = phase2.enter_context(tc.tile_pool(name="qpool", bufs=1))
+            scaled = {}
+
+            def scale(t):
+                yv = ypool.tile([P, V_COLS], F32, name="yv")
+                ys = ypool.tile([P, WIDTH - V_COLS], F32, name="ys")
+                nc.vector.tensor_scalar(out=yv[:], in0=o_sb[t][:, 0:V_COLS], scalar1=inverse, scalar2=448.0, op0=ALU.mult, op1=ALU.mult)
+                nc.scalar.activation(out=ys[:], in_=o_sb[t][:, V_COLS:WIDTH], func=ACT.Copy, scale=inverse)
+                scaled[t] = (yv, ys)
+
+            def cast(t):
+                yv, ys = scaled[t]
+                q8 = qpool.tile([P, WIDTH], FP8, name="q%d" % t)
+                nc.vector.tensor_copy(out=q8[:, 0:V_COLS], in_=yv[:], saturate=False)
+                nc.scalar.activation(out=q8[:, V_COLS:WIDTH], in_=ys[:], func=ACT.Copy, scale=448.0, saturate=False)
+                nc.sync.dma_start(out=o1[t * P : (t + 1) * P, :], in_=q8[:].bitcast(U8))
+
+            scale(0)
+            for t in range(N_TILES):
+                if t + 1 < N_TILES:
+                    scale(t + 1)
+                cast(t)

@@ -29,20 +29,36 @@ K = 3
 NI = 4
 NJ = 5
 NK = 6
-WINDOWS = ((R, I, J, K), (NI, R, I, NI), (NJ, NJ, R, J), (NK, K, NK, R))
+CODE_BLOCKS = (NI, R, I, NI, NK, K, NK, R, J, K, NJ, NJ)
+FIRST_BLOCK = ((1, 8), (0, 2), (10, 7), (4, 6))
+HALF = 256
 
 V_HELP_TILES = 0
 V_COLS = 1376
-SG_FROM = 8
+SG_FROM = 99
 SG_MOD = 2
-SG_LAST = 29
-G_NEG_FROM = 1
-PEND_PER = 2
-ORDER = [("w", 0), ("x", 0), ("x", 1), ("x", 2), ("x", 3), ("w", 1), ("x", 4), ("x", 5), ("x", 6), ("x", 7), ("w", 2), ("w", 3)]
+SG_LAST = 0
+G_NEG_FROM = 2
+PEND_PER = 5
+ORDER = [("w", 0), ("x", 0), ("w", 1), ("x", 1), ("x", 2), ("w", 2), ("x", 3), ("w", 3), ("x", 4), ("x", 5), ("x", 6), ("x", 7)]
+
+
+def singles(banks):
+    return [(c, 1, t) for c, t in banks]
+
+
+def pairs(banks):
+    out = []
+    for c, t in banks:
+        if out and out[-1][2] == t and out[-1][0] + out[-1][1] == c:
+            out[-1] = (out[-1][0], out[-1][1] + 1, t)
+        else:
+            out.append((c, 1, t))
+    return out
 
 
 def quantize_runs():
-    flat = [b for win in WINDOWS for b in win]
+    flat = list(CODE_BLOCKS)
     runs = []
     d = 0
     while d < len(flat):
@@ -75,12 +91,13 @@ def tile_quaternionlinear_pa_kernel(tc, x, wr, wi, wj, wk, bias, out_0, out_1):
         bias_row = const.tile([P, WIDTH], BF16, name="bias_row")
         bias_sb = const.tile([P, WIDTH], BF16, name="bias_sb")
         stats = const.tile([P, N_TILES * O_CHUNKS], F32, name="stats")
+        nc.vector.memset(stats[:], 0.0)
         small = const.tile([P, 8], F32, name="small")
 
         x_codes = [keep.tile([P, Q * P], U32, name="xc%d" % t, align_bytes=64) for t in range(N_TILES)]
         x_scales = [keep.tile([P, Q * P], U8, name="xs%d" % t, align_bytes=64) for t in range(N_TILES)]
-        w_codes = [keep.tile([P, Q * BANK], U32, name="wc%d" % c, align_bytes=64) for c in range(O_CHUNKS)]
-        w_scales = [keep.tile([P, Q * BANK], U8, name="ws%d" % c, align_bytes=64) for c in range(O_CHUNKS)]
+        w_codes = [keep.tile([P, len(CODE_BLOCKS) * P], U32, name="wc%d" % c, align_bytes=64) for c in range(O_CHUNKS)]
+        w_scales = [keep.tile([P, len(CODE_BLOCKS) * P], U8, name="ws%d" % c, align_bytes=64) for c in range(O_CHUNKS)]
         o_sb = [keep.tile([P, WIDTH], F32, name="o%d" % t) for t in range(N_TILES)]
 
         with ExitStack() as phase1:
@@ -112,13 +129,19 @@ def tile_quaternionlinear_pa_kernel(tc, x, wr, wi, wj, wk, bias, out_0, out_1):
                 else:
                     load_x(n)
 
+            bias_banks = []
+
             def spread_bias():
                 for h in range(2):
                     bp = psum.tile([P, 2 * BANK], BF16, name="bank")
                     for e in range(2):
                         cols = slice((2 * h + e) * BANK, (2 * h + e + 1) * BANK)
                         nc.tensor.matmul(out=bp[:, e * BANK : (e + 1) * BANK], lhsT=ones[:], rhs=bias_row[:, cols], start=True, stop=True)
-                    nc.vector.tensor_copy(out=bias_sb[:, 2 * h * BANK : 2 * (h + 1) * BANK], in_=bp[:])
+                    bias_banks.append(bp)
+
+            def copy_bias():
+                for h in range(2):
+                    nc.vector.tensor_copy(out=bias_sb[:, 2 * h * BANK : 2 * (h + 1) * BANK], in_=bias_banks[h][:])
 
             banks_t = {}
             grouped = {}
@@ -150,7 +173,7 @@ def tile_quaternionlinear_pa_kernel(tc, x, wr, wi, wj, wk, bias, out_0, out_1):
                             in_=pts[h][:].rearrange("p y u o -> p y o u"),
                         )
                     if n >= G_NEG_FROM:
-                        nc.gpsimd.tensor_scalar(out=wg[:, NI : NK + 1, :], in0=wg[:, I : K + 1, :], scalar1=-1.0, scalar2=0.0, op0=ALU.mult, op1=ALU.add)
+                        nc.scalar.activation(out=wg[:, NI : NK + 1, :], in_=wg[:, I : K + 1, :], func=ACT.Copy, scale=-1.0)
                     grouped[(kind, n)] = wg
                 else:
                     xg = stage.tile([P, Q, P, 4], BF16, name="xg", bufs=3, align_bytes=64)
@@ -186,88 +209,90 @@ def tile_quaternionlinear_pa_kernel(tc, x, wr, wi, wj, wk, bias, out_0, out_1):
                     steps.append(one(s, cnt, d))
                 return steps
 
-            all_banks = [(c, t) for c in range(O_CHUNKS) for t in range(N_TILES)]
-            n_banks = len(all_banks)
             acc_of = {}
-            due = {}
+            n_stats = [0]
 
-            def by_scalar_and_gpsimd(i):
-                return SG_FROM <= i <= SG_LAST and i % SG_MOD == 0
-
-            def multiply(i):
-                c, t = all_banks[i]
+            def multiply(c, t):
                 acc = psum.tile([P, BANK], F32, name="bank")
-                for comp in range(Q):
-                    nc.tensor.matmul_mx(
-                        out=acc[:],
-                        lhsT=x_codes[t][:, comp * P : (comp + 1) * P].bitcast(FP8X4),
-                        lhsT_scale=x_scales[t][:, comp * P : (comp + 1) * P],
-                        rhs=w_codes[c][:, comp * BANK : (comp + 1) * BANK].bitcast(FP8X4),
-                        rhs_scale=w_scales[c][:, comp * BANK : (comp + 1) * BANK],
-                        start=(comp == 0),
-                        stop=(comp == Q - 1),
-                    )
-                acc_of[i] = acc
+                for h in range(2):
+                    for comp in range(Q):
+                        first = FIRST_BLOCK[comp][h] * P
+                        nc.tensor.matmul_mx(
+                            out=acc[:, h * HALF : (h + 1) * HALF],
+                            lhsT=x_codes[t][:, comp * P : (comp + 1) * P].bitcast(FP8X4),
+                            lhsT_scale=x_scales[t][:, comp * P : (comp + 1) * P],
+                            rhs=w_codes[c][:, first : first + HALF].bitcast(FP8X4),
+                            rhs_scale=w_scales[c][:, first : first + HALF],
+                            start=(comp == 0),
+                            stop=(comp == Q - 1),
+                        )
+                acc_of[(c, t)] = acc
 
-            def add_bias(i):
-                c, t = all_banks[i]
+            def add_bias(c, t):
                 cols = slice(c * BANK, (c + 1) * BANK)
-                sums = acc_of[i][:].rearrange("p (c o) -> p o c", c=Q)
-                if by_scalar_and_gpsimd(i):
-                    plain = stage.tile([P, BANK], F32, name="plain", bufs=3)
-                    nc.scalar.copy(out=plain[:].rearrange("p (o c) -> p o c", c=Q), in_=sums)
-                    nc.gpsimd.tensor_tensor(out=o_sb[t][:, cols], in0=plain[:], in1=bias_sb[:, cols], op=ALU.add)
-                else:
-                    nc.vector.tensor_tensor(
-                        out=o_sb[t][:, cols].rearrange("p (o c) -> p o c", c=Q),
-                        in0=sums,
-                        in1=bias_sb[:, cols].rearrange("p (o c) -> p o c", c=Q),
-                        op=ALU.add,
-                    )
-                nc.sync.dma_start(out=o0[t * P : (t + 1) * P, cols], in_=o_sb[t][:, cols])
-
-            def abs_max(i):
-                c, t = all_banks[i]
-                nc.vector.tensor_reduce(
-                    out=stats[:, i : i + 1], in_=o_sb[t][:, c * BANK : (c + 1) * BANK], axis=AXIS_X, op=ALU.max, apply_absolute_value=True
+                nc.vector.tensor_tensor(
+                    out=o_sb[t][:, cols].rearrange("p (o c) -> p o c", c=Q),
+                    in0=acc_of[(c, t)][:].rearrange("p (c o) -> p o c", c=Q),
+                    in1=bias_sb[:, cols].rearrange("p (o c) -> p o c", c=Q),
+                    op=ALU.add,
                 )
 
-            def bank_step(i):
-                if i < n_banks:
-                    multiply(i)
-                if 1 <= i <= n_banks:
-                    add_bias(i - 1)
-                    lag = 3 if by_scalar_and_gpsimd(i - 1) else 1
-                    due.setdefault(i + lag, []).append(i - 1)
-                for b in due.get(i, []):
-                    abs_max(b)
+            def finish(c0, n, t):
+                cols = slice(c0 * BANK, (c0 + n) * BANK)
+                nc.sync.dma_start(out=o0[t * P : (t + 1) * P, cols], in_=o_sb[t][:, cols])
+                nc.vector.tensor_reduce(out=stats[:, n_stats[0] : n_stats[0] + 1], in_=o_sb[t][:, cols], axis=AXIS_X, op=ALU.max, apply_absolute_value=True)
+                n_stats[0] += 1
 
-            transposes(*order[0])
-            transposes(*order[1])
+            PLAN = [("T", "w", 0), ("T", "x", 0), ("E", "w", 0), ("T", "w", 1), ("T", "b", 0), ("E", "x", 0), ("E", "b", 0), ("T", "x", 1), ("M", 0, 0), ("E", "w", 1), ("E", "x", 1), ("T", "x", 2), ("T", "w", 2), ("M", 0, 1), ("M", 1, 0), ("M", 1, 1), ("E", "x", 2), ("E", "w", 2), ("T", "x", 3), ("T", "w", 3), ("M", 0, 2), ("M", 1, 2), ("E", "x", 3), ("E", "w", 3), ("M", 0, 3), ("M", 1, 3), ("M", 2, 0), ("M", 3, 0), ("M", 2, 1), ("M", 3, 1), ("T", "x", 4), ("M", 2, 2), ("M", 3, 2), ("E", "x", 4), ("M", 2, 3), ("M", 3, 3), ("T", "x", 5), ("M", 0, 4), ("M", 1, 4), ("E", "x", 5), ("M", 2, 4), ("M", 3, 4), ("T", "x", 6), ("M", 0, 5), ("M", 1, 5), ("E", "x", 6), ("M", 2, 5), ("M", 3, 5), ("T", "x", 7), ("M", 0, 6), ("M", 1, 6), ("E", "x", 7), ("M", 2, 6), ("M", 3, 6), ("M", 0, 7), ("M", 1, 7), ("M", 2, 7), ("M", 3, 7)]
+            waiting = []
+            groups = []
             pending = []
-            issued = 0
-            done = 0
-            for j in range(len(order)):
-                kind, n = order[j]
-                empty(kind, n)
-                if j == 1:
-                    spread_bias()
-                if j + 2 < len(order):
-                    transposes(*order[j + 2])
-                if kind == "w" and n >= 2:
-                    pending.extend(quantize_steps(kind, n))
-                else:
-                    for step in quantize_steps(kind, n):
-                        step()
-                if kind == "x":
-                    bank_step(done)
-                    done += 1
-            while done < n_banks + 5:
-                bank_step(done)
-                done += 1
-                for step in pending[issued : issued + PEND_PER]:
+            state = {"issued": 0}
+
+            def some_pending(n):
+                for step in pending[state["issued"] : state["issued"] + n]:
                     step()
-                issued += PEND_PER
+                state["issued"] = min(state["issued"] + n, len(pending))
+
+            def retire(keep_banks, keep_groups):
+                while len(waiting) > keep_banks:
+                    c, t = waiting[0]
+                    waiting.remove((c, t))
+                    add_bias(c, t)
+                    if groups and groups[-1][2] == t and groups[-1][0] + groups[-1][1] == c and groups[-1][1] < 2 and (c, t) != (O_CHUNKS - 1, N_TILES - 1):
+                        groups[-1] = (groups[-1][0], groups[-1][1] + 1, t)
+                    else:
+                        groups.append((c, 1, t))
+                    while len(groups) > keep_groups or (groups and groups[0][1] == 2 and True):
+                        finish(*groups[0])
+                        groups.remove(groups[0])
+                if keep_groups == 0:
+                    while groups:
+                        finish(*groups[0])
+                        groups.remove(groups[0])
+
+            for op in PLAN:
+                if op[0] == "T":
+                    if op[1] == "b":
+                        spread_bias()
+                    else:
+                        transposes(op[1], op[2])
+                elif op[0] == "E":
+                    if op[1] == "b":
+                        copy_bias()
+                    else:
+                        empty(op[1], op[2])
+                        if op[1] == "w" and op[2] >= 2:
+                            pending.extend(quantize_steps(op[1], op[2]))
+                        else:
+                            for step in quantize_steps(op[1], op[2]):
+                                step()
+                else:
+                    multiply(op[1], op[2])
+                    waiting.append((op[1], op[2]))
+                    retire(1, 1)
+                    some_pending(PEND_PER)
+            retire(0, 0)
 
         nc.vector.tensor_reduce(out=small[:, 2:3], in_=stats[:], axis=AXIS_X, op=ALU.max)
         spread = psum.tile([P, P], F32, name="bank")

@@ -29,17 +29,16 @@ K = 3
 NI = 4
 NJ = 5
 NK = 6
-CODE_BLOCKS = (NI, R, I, NI, NK, K, NK, R, J, K, NJ, NJ)
-FIRST_BLOCK = ((1, 8), (0, 2), (10, 7), (4, 6))
-HALF = 256
+WINDOWS = ((R, I, J, K), (NI, R, I, NI), (NJ, NJ, R, J), (NK, K, NK, R))
+CODE_BLOCKS = tuple(b for win in WINDOWS for b in win)
 
 V_HELP_TILES = 0
 V_COLS = 1376
-SG_FROM = 99
+SG_FROM = 8
 SG_MOD = 2
-SG_LAST = 0
+SG_LAST = 29
 G_NEG_FROM = 2
-PEND_PER = 5
+PEND_PER = 6
 ORDER = [("w", 0), ("x", 0), ("w", 1), ("x", 1), ("x", 2), ("w", 2), ("x", 3), ("w", 3), ("x", 4), ("x", 5), ("x", 6), ("x", 7)]
 
 
@@ -145,6 +144,18 @@ def tile_quaternionlinear_pa_kernel(tc, x, wr, wi, wj, wk, bias, out_0, out_1):
 
             banks_t = {}
             grouped = {}
+            sorted_x = {}
+
+            def sort_x(n):
+                xs = stage.tile([P, Q, 512], BF16, name="xs", bufs=3)
+                src = x_raw[n][:].rearrange("r (p u e c) -> r c u p e", u=2, e=2, c=Q)
+                for c in range(Q):
+                    dst = xs[:, c, :].rearrange("r (u p e) -> r u p e", u=2, e=2)
+                    if c in (2, 3):
+                        nc.gpsimd.tensor_scalar(out=dst, in0=src[:, c], scalar1=1.0, scalar2=0.0, op0=ALU.mult, op1=ALU.add)
+                    else:
+                        nc.scalar.copy(out=dst, in_=src[:, c])
+                sorted_x[n] = xs
 
             def transposes(kind, n):
                 pts = []
@@ -156,10 +167,11 @@ def tile_quaternionlinear_pa_kernel(tc, x, wr, wi, wj, wk, bias, out_0, out_1):
                             for u in range(2):
                                 nc.tensor.transpose(pt[:, yy, u, :], words[:, u::2], ident_f[:])
                     else:
-                        pt = psum.tile([P, 8, P], BF16, name="bank")
+                        pt = psum.tile([P, 4, P], F32, name="bank")
                         for cc in range(2):
-                            for t in range(4):
-                                nc.tensor.transpose(pt[:, cc * 4 + t, :], x_raw[n][:, 4 * t + 2 * h + cc :: 16], ident_b[:])
+                            words = sorted_x[n][:, 2 * h + cc, :].bitcast(F32)
+                            for u in range(2):
+                                nc.tensor.transpose(pt[:, cc * 2 + u, :], words[:, u * P : (u + 1) * P], ident_f[:])
                     pts.append(pt)
                 banks_t[(kind, n)] = pts
 
@@ -178,11 +190,10 @@ def tile_quaternionlinear_pa_kernel(tc, x, wr, wi, wj, wk, bias, out_0, out_1):
                 else:
                     xg = stage.tile([P, Q, P, 4], BF16, name="xg", bufs=3, align_bytes=64)
                     for h in range(2):
-                        src = pts[h][:].rearrange("p (c t) n -> p c n t", c=2)
-                        if h == 1 and n < V_HELP_TILES:
-                            nc.vector.tensor_copy(out=xg[:, 2 * h : 2 * h + 2, :, :], in_=src)
-                        else:
-                            nc.scalar.copy(out=xg[:, 2 * h : 2 * h + 2, :, :], in_=src)
+                        nc.scalar.copy(
+                            out=xg[:, 2 * h : 2 * h + 2, :, :].rearrange("p c n t -> p c (n t)").bitcast(F32).rearrange("p c (n u) -> p c n u", u=2),
+                            in_=pts[h][:].rearrange("p (c u) n -> p c n u", c=2),
+                        )
                     grouped[(kind, n)] = xg
 
             def quantize_steps(kind, n):
@@ -214,28 +225,32 @@ def tile_quaternionlinear_pa_kernel(tc, x, wr, wi, wj, wk, bias, out_0, out_1):
 
             def multiply(c, t):
                 acc = psum.tile([P, BANK], F32, name="bank")
-                for h in range(2):
-                    for comp in range(Q):
-                        first = FIRST_BLOCK[comp][h] * P
-                        nc.tensor.matmul_mx(
-                            out=acc[:, h * HALF : (h + 1) * HALF],
-                            lhsT=x_codes[t][:, comp * P : (comp + 1) * P].bitcast(FP8X4),
-                            lhsT_scale=x_scales[t][:, comp * P : (comp + 1) * P],
-                            rhs=w_codes[c][:, first : first + HALF].bitcast(FP8X4),
-                            rhs_scale=w_scales[c][:, first : first + HALF],
-                            start=(comp == 0),
-                            stop=(comp == Q - 1),
-                        )
+                for comp in range(Q):
+                    nc.tensor.matmul_mx(
+                        out=acc[:],
+                        lhsT=x_codes[t][:, comp * P : (comp + 1) * P].bitcast(FP8X4),
+                        lhsT_scale=x_scales[t][:, comp * P : (comp + 1) * P],
+                        rhs=w_codes[c][:, comp * BANK : (comp + 1) * BANK].bitcast(FP8X4),
+                        rhs_scale=w_scales[c][:, comp * BANK : (comp + 1) * BANK],
+                        start=(comp == 0),
+                        stop=(comp == Q - 1),
+                    )
                 acc_of[(c, t)] = acc
 
-            def add_bias(c, t):
+            def add_bias(c, t, helped):
                 cols = slice(c * BANK, (c + 1) * BANK)
-                nc.vector.tensor_tensor(
-                    out=o_sb[t][:, cols].rearrange("p (o c) -> p o c", c=Q),
-                    in0=acc_of[(c, t)][:].rearrange("p (c o) -> p o c", c=Q),
-                    in1=bias_sb[:, cols].rearrange("p (o c) -> p o c", c=Q),
-                    op=ALU.add,
-                )
+                sums = acc_of[(c, t)][:].rearrange("p (c o) -> p o c", c=Q)
+                if helped:
+                    plain = stage.tile([P, BANK], F32, name="plain", bufs=3)
+                    nc.scalar.copy(out=plain[:].rearrange("p (o c) -> p o c", c=Q), in_=sums)
+                    nc.gpsimd.tensor_tensor(out=o_sb[t][:, cols], in0=plain[:], in1=bias_sb[:, cols], op=ALU.add)
+                else:
+                    nc.vector.tensor_tensor(
+                        out=o_sb[t][:, cols].rearrange("p (o c) -> p o c", c=Q),
+                        in0=sums,
+                        in1=bias_sb[:, cols].rearrange("p (o c) -> p o c", c=Q),
+                        op=ALU.add,
+                    )
 
             def finish(c0, n, t):
                 cols = slice(c0 * BANK, (c0 + n) * BANK)
@@ -243,36 +258,44 @@ def tile_quaternionlinear_pa_kernel(tc, x, wr, wi, wj, wk, bias, out_0, out_1):
                 nc.vector.tensor_reduce(out=stats[:, n_stats[0] : n_stats[0] + 1], in_=o_sb[t][:, cols], axis=AXIS_X, op=ALU.max, apply_absolute_value=True)
                 n_stats[0] += 1
 
-            PLAN = [("T", "w", 0), ("T", "x", 0), ("E", "w", 0), ("T", "w", 1), ("T", "b", 0), ("E", "x", 0), ("E", "b", 0), ("T", "x", 1), ("M", 0, 0), ("E", "w", 1), ("E", "x", 1), ("T", "x", 2), ("T", "w", 2), ("M", 0, 1), ("M", 1, 0), ("M", 1, 1), ("E", "x", 2), ("E", "w", 2), ("T", "x", 3), ("T", "w", 3), ("M", 0, 2), ("M", 1, 2), ("E", "x", 3), ("E", "w", 3), ("M", 0, 3), ("M", 1, 3), ("M", 2, 0), ("M", 3, 0), ("M", 2, 1), ("M", 3, 1), ("T", "x", 4), ("M", 2, 2), ("M", 3, 2), ("E", "x", 4), ("M", 2, 3), ("M", 3, 3), ("T", "x", 5), ("M", 0, 4), ("M", 1, 4), ("E", "x", 5), ("M", 2, 4), ("M", 3, 4), ("T", "x", 6), ("M", 0, 5), ("M", 1, 5), ("E", "x", 6), ("M", 2, 5), ("M", 3, 5), ("T", "x", 7), ("M", 0, 6), ("M", 1, 6), ("E", "x", 7), ("M", 2, 6), ("M", 3, 6), ("M", 0, 7), ("M", 1, 7), ("M", 2, 7), ("M", 3, 7)]
+            PLAN = [("T", "w", 0), ("E", "w", 0), ("S", "x", 0), ("T", "x", 0), ("T", "w", 1), ("T", "b", 0), ("S", "x", 1), ("E", "x", 0), ("E", "b", 0), ("E", "w", 1), ("T", "x", 1), ("M", 0, 0), ("S", "x", 2), ("E", "x", 1), ("T", "x", 2), ("T", "w", 2), ("M", 1, 0), ("M", 0, 1), ("M", 1, 1), ("S", "x", 3), ("E", "x", 2), ("E", "w", 2), ("T", "x", 3), ("T", "w", 3), ("M", 0, 2), ("M", 1, 2), ("E", "x", 3), ("E", "w", 3), ("S", "x", 4), ("M", 0, 3), ("M", 1, 3), ("M", 2, 0), ("M", 3, 0), ("T", "x", 4), ("M", 2, 1), ("M", 3, 1), ("E", "x", 4), ("S", "x", 5), ("M", 2, 2), ("M", 3, 2), ("M", 2, 3), ("M", 3, 3), ("T", "x", 5), ("M", 0, 4), ("M", 1, 4), ("E", "x", 5), ("S", "x", 6), ("M", 2, 4), ("M", 3, 4), ("T", "x", 6), ("M", 0, 5), ("M", 1, 5), ("E", "x", 6), ("S", "x", 7), ("M", 2, 5), ("M", 3, 5), ("T", "x", 7), ("M", 0, 6), ("M", 1, 6), ("E", "x", 7), ("M", 2, 6), ("M", 3, 6), ("M", 0, 7), ("M", 1, 7), ("M", 2, 7), ("M", 3, 7)]
+            n_mult = len([op for op in PLAN if op[0] == "M"])
             waiting = []
             groups = []
             pending = []
-            state = {"issued": 0}
+            state = {"issued": 0, "retired": 0}
 
             def some_pending(n):
                 for step in pending[state["issued"] : state["issued"] + n]:
                     step()
                 state["issued"] = min(state["issued"] + n, len(pending))
 
-            def retire(keep_banks, keep_groups):
+            def retire(keep_banks, flush):
                 while len(waiting) > keep_banks:
                     c, t = waiting[0]
                     waiting.remove((c, t))
-                    add_bias(c, t)
-                    if groups and groups[-1][2] == t and groups[-1][0] + groups[-1][1] == c and groups[-1][1] < 2 and (c, t) != (O_CHUNKS - 1, N_TILES - 1):
-                        groups[-1] = (groups[-1][0], groups[-1][1] + 1, t)
+                    k = state["retired"]
+                    helped = SG_FROM <= k <= SG_LAST and k % SG_MOD == 0
+                    add_bias(c, t, helped)
+                    state["retired"] = k + 1
+                    ready = k + 1 + (3 if helped else 0)
+                    g = groups[-1] if groups else None
+                    if g and g[2] == t and g[0] + g[1] == c and g[1] < 2 and k < n_mult - 1:
+                        groups[-1] = [g[0], g[1] + 1, t, max(g[3], ready)]
                     else:
-                        groups.append((c, 1, t))
-                    while len(groups) > keep_groups or (groups and groups[0][1] == 2 and True):
-                        finish(*groups[0])
+                        groups.append([c, 1, t, ready])
+                    while groups and groups[0][3] <= state["retired"] and (len(groups) > 1 or groups[0][1] == 2):
+                        finish(groups[0][0], groups[0][1], groups[0][2])
                         groups.remove(groups[0])
-                if keep_groups == 0:
+                if flush:
                     while groups:
-                        finish(*groups[0])
+                        finish(groups[0][0], groups[0][1], groups[0][2])
                         groups.remove(groups[0])
 
             for op in PLAN:
-                if op[0] == "T":
+                if op[0] == "S":
+                    sort_x(op[2])
+                elif op[0] == "T":
                     if op[1] == "b":
                         spread_bias()
                     else:
@@ -290,9 +313,9 @@ def tile_quaternionlinear_pa_kernel(tc, x, wr, wi, wj, wk, bias, out_0, out_1):
                 else:
                     multiply(op[1], op[2])
                     waiting.append((op[1], op[2]))
-                    retire(1, 1)
+                    retire(1, False)
                     some_pending(PEND_PER)
-            retire(0, 0)
+            retire(0, True)
 
         nc.vector.tensor_reduce(out=small[:, 2:3], in_=stats[:], axis=AXIS_X, op=ALU.max)
         spread = psum.tile([P, P], F32, name="bank")

@@ -109,7 +109,6 @@ def tile_quaternionlinear_pa_kernel(tc, x, wr, wi, wj, wk, bias, out_0, out_1):
             nc.vector.memset(bias_row[:], 0.0)
             nc.vector.memset(ones[:], 1.0)
             nc.vector.memset(small[:], 1.0)
-            nc.scalar.dma_start(out=bias_row[0:1, :], in_=bias.rearrange("(a n) -> a n", a=1))
             nc.scalar.activation(out=small[:, 1:2], in_=small[:, 0:1], func=ACT.Copy)
             masks.make_identity(nc, ident_f[:])
             masks.make_identity(nc, ident_b[:])
@@ -122,7 +121,10 @@ def tile_quaternionlinear_pa_kernel(tc, x, wr, wi, wj, wk, bias, out_0, out_1):
                 nc.sync.dma_start(out=x_raw[t][:], in_=xf[t * P : (t + 1) * P, :])
 
             order = ORDER
-            for kind, n in order:
+            for j in range(len(order)):
+                kind, n = order[j]
+                if j == 2:
+                    nc.sync.dma_start(out=bias_row[0:1, :], in_=bias.rearrange("(a n) -> a n", a=1))
                 if kind == "w":
                     load_w(n)
                 else:
@@ -252,13 +254,21 @@ def tile_quaternionlinear_pa_kernel(tc, x, wr, wi, wj, wk, bias, out_0, out_1):
                         op=ALU.add,
                     )
 
+            backlog = []
+
             def finish(c0, n, t):
                 cols = slice(c0 * BANK, (c0 + n) * BANK)
                 nc.sync.dma_start(out=o0[t * P : (t + 1) * P, cols], in_=o_sb[t][:, cols])
-                nc.vector.tensor_reduce(out=stats[:, n_stats[0] : n_stats[0] + 1], in_=o_sb[t][:, cols], axis=AXIS_X, op=ALU.max, apply_absolute_value=True)
-                n_stats[0] += 1
+                backlog.append((c0, n, t))
 
-            PLAN = [("T", "w", 0), ("E", "w", 0), ("S", "x", 0), ("T", "x", 0), ("T", "w", 1), ("T", "b", 0), ("S", "x", 1), ("E", "x", 0), ("E", "b", 0), ("E", "w", 1), ("T", "x", 1), ("M", 0, 0), ("S", "x", 2), ("E", "x", 1), ("T", "x", 2), ("T", "w", 2), ("M", 1, 0), ("M", 0, 1), ("M", 1, 1), ("S", "x", 3), ("E", "x", 2), ("E", "w", 2), ("T", "x", 3), ("T", "w", 3), ("M", 0, 2), ("M", 1, 2), ("E", "x", 3), ("E", "w", 3), ("S", "x", 4), ("M", 0, 3), ("M", 1, 3), ("M", 2, 0), ("M", 3, 0), ("T", "x", 4), ("M", 2, 1), ("M", 3, 1), ("E", "x", 4), ("S", "x", 5), ("M", 2, 2), ("M", 3, 2), ("M", 2, 3), ("M", 3, 3), ("T", "x", 5), ("M", 0, 4), ("M", 1, 4), ("E", "x", 5), ("S", "x", 6), ("M", 2, 4), ("M", 3, 4), ("T", "x", 6), ("M", 0, 5), ("M", 1, 5), ("E", "x", 6), ("S", "x", 7), ("M", 2, 5), ("M", 3, 5), ("T", "x", 7), ("M", 0, 6), ("M", 1, 6), ("E", "x", 7), ("M", 2, 6), ("M", 3, 6), ("M", 0, 7), ("M", 1, 7), ("M", 2, 7), ("M", 3, 7)]
+            def abs_max(count):
+                for c0, n, t in backlog[:count]:
+                    cols = slice(c0 * BANK, (c0 + n) * BANK)
+                    nc.vector.tensor_reduce(out=stats[:, n_stats[0] : n_stats[0] + 1], in_=o_sb[t][:, cols], axis=AXIS_X, op=ALU.max, apply_absolute_value=True)
+                    n_stats[0] += 1
+                    backlog.remove((c0, n, t))
+
+            PLAN = [("T", "w", 0), ("E", "w", 0), ("T", "b", 0), ("S", "x", 0), ("T", "x", 0), ("T", "w", 1), ("E", "x", 0), ("S", "x", 1), ("E", "b", 0), ("E", "w", 1), ("M", 0, 0), ("T", "x", 1), ("S", "x", 2), ("E", "x", 1), ("T", "x", 2), ("T", "w", 2), ("M", 1, 0), ("M", 0, 1), ("M", 1, 1), ("S", "x", 3), ("E", "x", 2), ("E", "w", 2), ("T", "x", 3), ("T", "w", 3), ("M", 0, 2), ("E", "x", 3), ("M", 1, 2), ("E", "w", 3), ("S", "x", 4), ("M", 0, 3), ("M", 1, 3), ("M", 2, 0), ("S", "x", 5), ("M", 3, 0), ("M", 2, 1), ("M", 3, 1), ("T", "x", 4), ("T", "x", 5), ("M", 2, 2), ("E", "x", 4), ("M", 3, 2), ("E", "x", 5), ("S", "x", 6), ("M", 2, 3), ("S", "x", 7), ("M", 3, 3), ("M", 0, 4), ("M", 1, 4), ("M", 2, 4), ("M", 3, 4), ("T", "x", 6), ("T", "x", 7), ("M", 0, 5), ("E", "x", 6), ("M", 1, 5), ("E", "x", 7), ("M", 2, 5), ("M", 3, 5), ("M", 0, 6), ("M", 1, 6), ("M", 2, 6), ("M", 3, 6), ("M", 0, 7), ("M", 1, 7), ("M", 2, 7), ("M", 3, 7)]
             n_mult = len([op for op in PLAN if op[0] == "M"])
             waiting = []
             groups = []
@@ -275,16 +285,16 @@ def tile_quaternionlinear_pa_kernel(tc, x, wr, wi, wj, wk, bias, out_0, out_1):
                     c, t = waiting[0]
                     waiting.remove((c, t))
                     k = state["retired"]
-                    helped = SG_FROM <= k <= SG_LAST and k % SG_MOD == 0
+                    helped = 8 <= k <= 28 and k % 2 == 0
                     add_bias(c, t, helped)
                     state["retired"] = k + 1
-                    ready = k + 1 + (3 if helped else 0)
+                    ready = k + 1 + (2 if helped else 0)
                     g = groups[-1] if groups else None
-                    if g and g[2] == t and g[0] + g[1] == c and g[1] < 2 and k < n_mult - 1:
+                    if g and g[2] == t and g[0] + g[1] == c and g[1] < 2 and k < n_mult - 2:
                         groups[-1] = [g[0], g[1] + 1, t, max(g[3], ready)]
                     else:
                         groups.append([c, 1, t, ready])
-                    while groups and groups[0][3] <= state["retired"] and (len(groups) > 1 or groups[0][1] == 2):
+                    while groups and groups[0][3] <= state["retired"] and (len(groups) > 1 or groups[0][1] == 2 or k >= n_mult - 2):
                         finish(groups[0][0], groups[0][1], groups[0][2])
                         groups.remove(groups[0])
                 if flush:
@@ -315,7 +325,12 @@ def tile_quaternionlinear_pa_kernel(tc, x, wr, wi, wj, wk, bias, out_0, out_1):
                     waiting.append((op[1], op[2]))
                     retire(1, False)
                     some_pending(PEND_PER)
+                    if state["retired"] >= n_mult - 2 - 1:
+                        abs_max(len(backlog))
+                    elif state["retired"] >= 8:
+                        abs_max(1)
             retire(0, True)
+            abs_max(len(backlog))
 
         nc.vector.tensor_reduce(out=small[:, 2:3], in_=stats[:], axis=AXIS_X, op=ALU.max)
         spread = psum.tile([P, P], F32, name="bank")

@@ -17,54 +17,50 @@ AXIS_X = mybir.AxisListType.X
 
 P = 128
 Q = 4
+IQ = 512
 N_TILES = 8
-O_CHUNKS = 4
-BANK = 512
-WIDTH = 2048
+N_CHUNKS = 4
+BANK = Q * P
+WIDTH = N_CHUNKS * BANK
+N_BANKS = N_CHUNKS * N_TILES
 
-R = 0
-I = 1
-J = 2
-K = 3
-NI = 4
-NJ = 5
-NK = 6
-WINDOWS = ((R, I, J, K), (NI, R, I, NI), (NJ, NJ, R, J), (NK, K, NK, R))
-CODE_BLOCKS = tuple(b for win in WINDOWS for b in win)
+WR = 0
+WI = 1
+WJ = 2
+WK = 3
+NEG_WI = 4
+NEG_WJ = 5
+NEG_WK = 6
+MOVING = (
+    (WR, WI, WJ, WK),
+    (NEG_WI, WR, WI, NEG_WI),
+    (NEG_WJ, NEG_WJ, WR, WJ),
+    (NEG_WK, WK, NEG_WK, WR),
+)
 
-V_HELP_TILES = 0
+HELPED_FIRST = 8
+HELPED_LAST = 28
+HELPED_LAG = 2
+QUANTIZE_CALLS_A_BANK = 6
+REDUCE_FROM = 8
+LAST_ALONE = 2
+
 V_COLS = 1376
-SG_FROM = 8
-SG_MOD = 2
-SG_LAST = 29
-G_NEG_FROM = 2
-PEND_PER = 6
-ORDER = [("w", 0), ("x", 0), ("w", 1), ("x", 1), ("x", 2), ("w", 2), ("x", 3), ("w", 3), ("x", 4), ("x", 5), ("x", 6), ("x", 7)]
 
 
-def singles(banks):
-    return [(c, 1, t) for c, t in banks]
-
-
-def pairs(banks):
-    out = []
-    for c, t in banks:
-        if out and out[-1][2] == t and out[-1][0] + out[-1][1] == c:
-            out[-1] = (out[-1][0], out[-1][1] + 1, t)
-        else:
-            out.append((c, 1, t))
-    return out
+def helped(k):
+    return HELPED_FIRST <= k <= HELPED_LAST and (k % 2 == 0 or k % 8 == 3)
 
 
 def quantize_runs():
-    flat = list(CODE_BLOCKS)
+    flat = [block for row in MOVING for block in row]
     runs = []
     d = 0
     while d < len(flat):
         n = 1
-        for cand in (4, 2):
-            if d + cand <= len(flat) and all(flat[d + e] == flat[d] + e for e in range(cand)):
-                n = cand
+        for longer in (4, 2):
+            if d + longer <= len(flat) and all(flat[d + e] == flat[d] + e for e in range(longer)):
+                n = longer
                 break
         runs.append((flat[d], n, d))
         d += n
@@ -73,9 +69,9 @@ def quantize_runs():
 
 def tile_quaternionlinear_pa_kernel(tc, x, wr, wi, wj, wk, bias, out_0, out_1):
     nc = tc.nc
-    xf = x.flatten_outer_dims()
-    o0 = out_0.flatten_outer_dims()
-    o1 = out_1.flatten_outer_dims()
+    x_rows = x.flatten_outer_dims()
+    out_rows = out_0.flatten_outer_dims()
+    byte_rows = out_1.flatten_outer_dims()
     weights = (wr, wi, wj, wk)
 
     with ExitStack() as ctx:
@@ -84,152 +80,198 @@ def tile_quaternionlinear_pa_kernel(tc, x, wr, wi, wj, wk, bias, out_0, out_1):
         psum = ctx.enter_context(tc.psum_pool(name="psum", bufs=8))
         ctx.enter_context(tc.manual_schedule())
 
-        ident_f = const.tile([P, P], F32, name="ident_f")
-        ident_b = const.tile([P, P], BF16, name="ident_b")
+        identity = const.tile([P, P], F32, name="identity")
         ones = const.tile([P, P], BF16, name="ones")
         bias_row = const.tile([P, WIDTH], BF16, name="bias_row")
-        bias_sb = const.tile([P, WIDTH], BF16, name="bias_sb")
-        stats = const.tile([P, N_TILES * O_CHUNKS], F32, name="stats")
-        nc.vector.memset(stats[:], 0.0)
+        bias_all = const.tile([P, WIDTH], BF16, name="bias_all")
+        maxima = const.tile([P, N_BANKS], F32, name="maxima")
         small = const.tile([P, 8], F32, name="small")
 
         x_codes = [keep.tile([P, Q * P], U32, name="xc%d" % t, align_bytes=64) for t in range(N_TILES)]
         x_scales = [keep.tile([P, Q * P], U8, name="xs%d" % t, align_bytes=64) for t in range(N_TILES)]
-        w_codes = [keep.tile([P, len(CODE_BLOCKS) * P], U32, name="wc%d" % c, align_bytes=64) for c in range(O_CHUNKS)]
-        w_scales = [keep.tile([P, len(CODE_BLOCKS) * P], U8, name="ws%d" % c, align_bytes=64) for c in range(O_CHUNKS)]
-        o_sb = [keep.tile([P, WIDTH], F32, name="o%d" % t) for t in range(N_TILES)]
+        w_codes = [keep.tile([P, Q * BANK], U32, name="wc%d" % c, align_bytes=64) for c in range(N_CHUNKS)]
+        w_scales = [keep.tile([P, Q * BANK], U8, name="ws%d" % c, align_bytes=64) for c in range(N_CHUNKS)]
+        result = [keep.tile([P, WIDTH], F32, name="o%d" % t) for t in range(N_TILES)]
 
         with ExitStack() as phase1:
             raw = phase1.enter_context(tc.tile_pool(name="raw", bufs=1))
             stage = phase1.enter_context(tc.tile_pool(name="stage", bufs=3))
 
             x_raw = [raw.tile([P, WIDTH], BF16, name="xr%d" % t) for t in range(N_TILES)]
-            w_raw = [raw.tile([P, Q, 512], BF16, name="wr%d" % c) for c in range(O_CHUNKS)]
+            w_raw = [raw.tile([P, Q, IQ], BF16, name="wr%d" % c) for c in range(N_CHUNKS)]
 
+            nc.vector.memset(maxima[:], 0.0)
             nc.vector.memset(bias_row[:], 0.0)
             nc.vector.memset(ones[:], 1.0)
             nc.vector.memset(small[:], 1.0)
             nc.scalar.activation(out=small[:, 1:2], in_=small[:, 0:1], func=ACT.Copy)
-            masks.make_identity(nc, ident_f[:])
-            masks.make_identity(nc, ident_b[:])
+            masks.make_identity(nc, identity[:])
 
             def load_w(c):
                 for y in range(Q):
                     nc.sync.dma_start(out=w_raw[c][:, y, :], in_=weights[y][c * P : (c + 1) * P, :])
 
             def load_x(t):
-                nc.sync.dma_start(out=x_raw[t][:], in_=xf[t * P : (t + 1) * P, :])
+                nc.sync.dma_start(out=x_raw[t][:], in_=x_rows[t * P : (t + 1) * P, :])
 
-            order = ORDER
-            for j in range(len(order)):
-                kind, n = order[j]
-                if j == 2:
-                    nc.sync.dma_start(out=bias_row[0:1, :], in_=bias.rearrange("(a n) -> a n", a=1))
-                if kind == "w":
-                    load_w(n)
-                else:
-                    load_x(n)
+            load_w(0)
+            load_x(0)
+            nc.sync.dma_start(out=bias_row[0:1, :], in_=bias.rearrange("(a n) -> a n", a=1))
+            load_w(1)
+            load_x(1)
+            load_x(2)
+            load_w(2)
+            load_x(3)
+            load_w(3)
+            for t in range(4, N_TILES):
+                load_x(t)
 
             bias_banks = []
 
             def spread_bias():
                 for h in range(2):
-                    bp = psum.tile([P, 2 * BANK], BF16, name="bank")
+                    spread = psum.tile([P, 2 * BANK], BF16, name="bank")
                     for e in range(2):
                         cols = slice((2 * h + e) * BANK, (2 * h + e + 1) * BANK)
-                        nc.tensor.matmul(out=bp[:, e * BANK : (e + 1) * BANK], lhsT=ones[:], rhs=bias_row[:, cols], start=True, stop=True)
-                    bias_banks.append(bp)
+                        nc.tensor.matmul(out=spread[:, e * BANK : (e + 1) * BANK], lhsT=ones[:], rhs=bias_row[:, cols], start=True, stop=True)
+                    bias_banks.append(spread)
 
             def copy_bias():
                 for h in range(2):
-                    nc.vector.tensor_copy(out=bias_sb[:, 2 * h * BANK : 2 * (h + 1) * BANK], in_=bias_banks[h][:])
+                    nc.vector.tensor_copy(out=bias_all[:, 2 * h * BANK : 2 * (h + 1) * BANK], in_=bias_banks[h][:])
 
-            banks_t = {}
-            grouped = {}
             sorted_x = {}
+            turned = {}
 
-            def sort_x(n):
-                xs = stage.tile([P, Q, 512], BF16, name="xs", bufs=3)
-                src = x_raw[n][:].rearrange("r (p u e c) -> r c u p e", u=2, e=2, c=Q)
+            def sort_x(t):
+                tile = stage.tile([P, Q, IQ], BF16, name="xs", bufs=3)
+                source = x_raw[t][:].rearrange("r (p u e c) -> r c u p e", u=2, e=2, c=Q)
                 for c in range(Q):
-                    dst = xs[:, c, :].rearrange("r (u p e) -> r u p e", u=2, e=2)
-                    if c in (2, 3):
-                        nc.gpsimd.tensor_scalar(out=dst, in0=src[:, c], scalar1=1.0, scalar2=0.0, op0=ALU.mult, op1=ALU.add)
+                    target = tile[:, c, :].rearrange("r (u p e) -> r u p e", u=2, e=2)
+                    if c < 2:
+                        nc.scalar.copy(out=target, in_=source[:, c])
                     else:
-                        nc.scalar.copy(out=dst, in_=src[:, c])
-                sorted_x[n] = xs
+                        nc.gpsimd.tensor_scalar(out=target, in0=source[:, c], scalar1=1.0, scalar2=0.0, op0=ALU.mult, op1=ALU.add)
+                sorted_x[t] = tile
 
-            def transposes(kind, n):
-                pts = []
+            def transpose_x(t):
+                banks = []
                 for h in range(2):
-                    if kind == "w":
-                        pt = psum.tile([P, 2, 2, P], F32, name="bank")
-                        for yy in range(2):
-                            words = w_raw[n][:, 2 * h + yy, :].bitcast(F32)
-                            for u in range(2):
-                                nc.tensor.transpose(pt[:, yy, u, :], words[:, u::2], ident_f[:])
-                    else:
-                        pt = psum.tile([P, 4, P], F32, name="bank")
-                        for cc in range(2):
-                            words = sorted_x[n][:, 2 * h + cc, :].bitcast(F32)
-                            for u in range(2):
-                                nc.tensor.transpose(pt[:, cc * 2 + u, :], words[:, u * P : (u + 1) * P], ident_f[:])
-                    pts.append(pt)
-                banks_t[(kind, n)] = pts
+                    bank = psum.tile([P, 4, P], F32, name="bank")
+                    for cc in range(2):
+                        words = sorted_x[t][:, 2 * h + cc, :].bitcast(F32)
+                        for u in range(2):
+                            nc.tensor.transpose(bank[:, cc * 2 + u, :], words[:, u * P : (u + 1) * P], identity[:])
+                    banks.append(bank)
+                turned[("x", t)] = banks
 
-            def empty(kind, n):
-                pts = banks_t[(kind, n)]
-                if kind == "w":
-                    wg = stage.tile([P, 7, 512], BF16, name="wg", bufs=2, align_bytes=64)
-                    for h in range(2):
-                        nc.scalar.copy(
-                            out=wg[:, 2 * h : 2 * h + 2, :].bitcast(F32).rearrange("p y (o u) -> p y o u", u=2),
-                            in_=pts[h][:].rearrange("p y u o -> p y o u"),
-                        )
-                    if n >= G_NEG_FROM:
-                        nc.scalar.activation(out=wg[:, NI : NK + 1, :], in_=wg[:, I : K + 1, :], func=ACT.Copy, scale=-1.0)
-                    grouped[(kind, n)] = wg
-                else:
-                    xg = stage.tile([P, Q, P, 4], BF16, name="xg", bufs=3, align_bytes=64)
-                    for h in range(2):
-                        nc.scalar.copy(
-                            out=xg[:, 2 * h : 2 * h + 2, :, :].rearrange("p c n t -> p c (n t)").bitcast(F32).rearrange("p c (n u) -> p c n u", u=2),
-                            in_=pts[h][:].rearrange("p (c u) n -> p c n u", c=2),
-                        )
-                    grouped[(kind, n)] = xg
-
-            def quantize_steps(kind, n):
-                g = grouped[(kind, n)]
-                steps = []
-                if kind == "x":
-                    steps.append(
-                        lambda: nc.vector.quantize_mx(
-                            out=x_codes[n][:].bitcast(FP8X4), scales=x_scales[n][:], in_=g[:].rearrange("p c n t -> p (c n t)")
-                        )
+            def collect_x(t):
+                grouped = stage.tile([P, Q, P, 4], BF16, name="xg", bufs=3, align_bytes=64)
+                for h in range(2):
+                    nc.scalar.copy(
+                        out=grouped[:, 2 * h : 2 * h + 2, :, :].rearrange("p c n t -> p c (n t)").bitcast(F32).rearrange("p c (n u) -> p c n u", u=2),
+                        in_=turned[("x", t)][h][:].rearrange("p (c u) n -> p c n u", c=2),
                     )
-                    return steps
-                if n < G_NEG_FROM:
-                    steps.append(lambda: nc.vector.tensor_scalar(out=g[:, NI : NK + 1, :], in0=g[:, I : K + 1, :], scalar1=-1.0, scalar2=None, op0=ALU.mult))
+                nc.vector.quantize_mx(out=x_codes[t][:].bitcast(FP8X4), scales=x_scales[t][:], in_=grouped[:].rearrange("p c n t -> p (c n t)"))
 
-                def one(s, cnt, d):
+            later_calls = []
+
+            def transpose_w(c):
+                banks = []
+                for h in range(2):
+                    bank = psum.tile([P, 2, 2, P], F32, name="bank")
+                    for yy in range(2):
+                        words = w_raw[c][:, 2 * h + yy, :].bitcast(F32)
+                        for u in range(2):
+                            nc.tensor.transpose(bank[:, yy, u, :], words[:, u::2], identity[:])
+                    banks.append(bank)
+                turned[("w", c)] = banks
+
+            def collect_w(c):
+                grouped = stage.tile([P, 7, IQ], BF16, name="wg", bufs=2, align_bytes=64)
+                for h in range(2):
+                    nc.scalar.copy(
+                        out=grouped[:, 2 * h : 2 * h + 2, :].bitcast(F32).rearrange("p y (o u) -> p y o u", u=2),
+                        in_=turned[("w", c)][h][:].rearrange("p y u o -> p y o u"),
+                    )
+                plus = grouped[:, WI : WK + 1, :]
+                minus = grouped[:, NEG_WI : NEG_WK + 1, :]
+
+                def call(first, n, d):
                     return lambda: nc.vector.quantize_mx(
-                        out=w_codes[n][:, d * P : (d + cnt) * P].bitcast(FP8X4),
-                        scales=w_scales[n][:, d * P : (d + cnt) * P],
-                        in_=g[:, s : s + cnt, :].rearrange("p b e -> p (b e)"),
+                        out=w_codes[c][:, d * P : (d + n) * P].bitcast(FP8X4),
+                        scales=w_scales[c][:, d * P : (d + n) * P],
+                        in_=grouped[:, first : first + n, :].rearrange("p b e -> p (b e)"),
                     )
 
-                for s, cnt, d in quantize_runs():
-                    steps.append(one(s, cnt, d))
-                return steps
+                calls = [call(first, n, d) for first, n, d in quantize_runs()]
+                if c < 2:
+                    nc.vector.tensor_scalar(out=minus, in0=plus, scalar1=-1.0, scalar2=None, op0=ALU.mult)
+                    for one in calls:
+                        one()
+                else:
+                    nc.scalar.activation(out=minus, in_=plus, func=ACT.Copy, scale=-1.0)
+                    later_calls.extend(calls)
 
-            acc_of = {}
-            n_stats = [0]
+            sums_of = {}
+            multiplied = []
+            open_runs = []
+            unreduced = []
+            count = {"biased": 0, "calls": 0, "maxima": 0}
 
-            def multiply(c, t):
-                acc = psum.tile([P, BANK], F32, name="bank")
+            def add_bias(c, t, k):
+                cols = slice(c * BANK, (c + 1) * BANK)
+                sums = sums_of[(c, t)][:].rearrange("p (c o) -> p o c", c=Q)
+                if helped(k):
+                    plain = stage.tile([P, BANK], F32, name="plain", bufs=3)
+                    nc.scalar.copy(out=plain[:].rearrange("p (o c) -> p o c", c=Q), in_=sums)
+                    nc.gpsimd.tensor_tensor(out=result[t][:, cols], in0=plain[:], in1=bias_all[:, cols], op=ALU.add)
+                else:
+                    nc.vector.tensor_tensor(
+                        out=result[t][:, cols].rearrange("p (o c) -> p o c", c=Q),
+                        in0=sums,
+                        in1=bias_all[:, cols].rearrange("p (o c) -> p o c", c=Q),
+                        op=ALU.add,
+                    )
+
+            def store_ready_runs(everything):
+                while open_runs and (everything or (open_runs[0][3] <= count["biased"] and (len(open_runs) > 1 or open_runs[0][1] == 2 or count["biased"] > N_BANKS - LAST_ALONE))):
+                    c0, n, t = open_runs[0][:3]
+                    open_runs.remove(open_runs[0])
+                    cols = slice(c0 * BANK, (c0 + n) * BANK)
+                    nc.sync.dma_start(out=out_rows[t * P : (t + 1) * P, cols], in_=result[t][:, cols])
+                    unreduced.append((c0, n, t))
+
+            def retire_oldest():
+                c, t = multiplied[0]
+                multiplied.remove((c, t))
+                k = count["biased"]
+                add_bias(c, t, k)
+                count["biased"] = k + 1
+                ready = k + 1 + (HELPED_LAG if helped(k) else 0)
+                last = open_runs[-1] if open_runs else None
+                if last and last[2] == t and last[0] + last[1] == c and last[1] < 2 and k < N_BANKS - LAST_ALONE:
+                    open_runs[-1] = [last[0], 2, t, max(last[3], ready)]
+                else:
+                    open_runs.append([c, 1, t, ready])
+
+            def reduce_oldest(n):
+                for c0, chunks, t in unreduced[:n]:
+                    unreduced.remove((c0, chunks, t))
+                    nc.vector.tensor_reduce(
+                        out=maxima[:, count["maxima"] : count["maxima"] + 1],
+                        in_=result[t][:, c0 * BANK : (c0 + chunks) * BANK],
+                        axis=AXIS_X,
+                        op=ALU.max,
+                        apply_absolute_value=True,
+                    )
+                    count["maxima"] += 1
+
+            def bank(c, t):
+                sums = psum.tile([P, BANK], F32, name="bank")
                 for comp in range(Q):
                     nc.tensor.matmul_mx(
-                        out=acc[:],
+                        out=sums[:],
                         lhsT=x_codes[t][:, comp * P : (comp + 1) * P].bitcast(FP8X4),
                         lhsT_scale=x_scales[t][:, comp * P : (comp + 1) * P],
                         rhs=w_codes[c][:, comp * BANK : (comp + 1) * BANK].bitcast(FP8X4),
@@ -237,129 +279,110 @@ def tile_quaternionlinear_pa_kernel(tc, x, wr, wi, wj, wk, bias, out_0, out_1):
                         start=(comp == 0),
                         stop=(comp == Q - 1),
                     )
-                acc_of[(c, t)] = acc
+                sums_of[(c, t)] = sums
+                multiplied.append((c, t))
+                if len(multiplied) > 1:
+                    retire_oldest()
+                    store_ready_runs(False)
+                for one in later_calls[count["calls"] : count["calls"] + QUANTIZE_CALLS_A_BANK]:
+                    one()
+                count["calls"] = min(count["calls"] + QUANTIZE_CALLS_A_BANK, len(later_calls))
+                if count["biased"] >= N_BANKS - LAST_ALONE - 1:
+                    reduce_oldest(len(unreduced))
+                elif count["biased"] >= REDUCE_FROM:
+                    reduce_oldest(1)
 
-            def add_bias(c, t, helped):
-                cols = slice(c * BANK, (c + 1) * BANK)
-                sums = acc_of[(c, t)][:].rearrange("p (c o) -> p o c", c=Q)
-                if helped:
-                    plain = stage.tile([P, BANK], F32, name="plain", bufs=3)
-                    nc.scalar.copy(out=plain[:].rearrange("p (o c) -> p o c", c=Q), in_=sums)
-                    nc.gpsimd.tensor_tensor(out=o_sb[t][:, cols], in0=plain[:], in1=bias_sb[:, cols], op=ALU.add)
-                else:
-                    nc.vector.tensor_tensor(
-                        out=o_sb[t][:, cols].rearrange("p (o c) -> p o c", c=Q),
-                        in0=sums,
-                        in1=bias_sb[:, cols].rearrange("p (o c) -> p o c", c=Q),
-                        op=ALU.add,
-                    )
+            transpose_w(0)
+            collect_w(0)
+            spread_bias()
+            sort_x(0)
+            transpose_x(0)
+            transpose_w(1)
+            collect_x(0)
+            sort_x(1)
+            copy_bias()
+            collect_w(1)
+            bank(0, 0)
+            transpose_x(1)
+            sort_x(2)
+            collect_x(1)
+            transpose_x(2)
+            transpose_w(2)
+            bank(1, 0)
+            bank(0, 1)
+            bank(1, 1)
+            sort_x(3)
+            collect_x(2)
+            collect_w(2)
+            transpose_x(3)
+            transpose_w(3)
+            bank(0, 2)
+            collect_x(3)
+            bank(1, 2)
+            collect_w(3)
+            sort_x(4)
+            bank(0, 3)
+            bank(1, 3)
+            bank(2, 0)
+            sort_x(5)
+            bank(3, 0)
+            bank(2, 1)
+            bank(3, 1)
+            transpose_x(4)
+            transpose_x(5)
+            bank(2, 2)
+            collect_x(4)
+            bank(3, 2)
+            collect_x(5)
+            sort_x(6)
+            bank(2, 3)
+            sort_x(7)
+            bank(3, 3)
+            for c in range(N_CHUNKS):
+                bank(c, 4)
+            transpose_x(6)
+            transpose_x(7)
+            bank(0, 5)
+            collect_x(6)
+            bank(1, 5)
+            collect_x(7)
+            bank(2, 5)
+            bank(3, 5)
+            for t in (6, 7):
+                for c in range(N_CHUNKS):
+                    bank(c, t)
+            retire_oldest()
+            store_ready_runs(True)
+            reduce_oldest(len(unreduced))
 
-            backlog = []
-
-            def finish(c0, n, t):
-                cols = slice(c0 * BANK, (c0 + n) * BANK)
-                nc.sync.dma_start(out=o0[t * P : (t + 1) * P, cols], in_=o_sb[t][:, cols])
-                backlog.append((c0, n, t))
-
-            def abs_max(count):
-                for c0, n, t in backlog[:count]:
-                    cols = slice(c0 * BANK, (c0 + n) * BANK)
-                    nc.vector.tensor_reduce(out=stats[:, n_stats[0] : n_stats[0] + 1], in_=o_sb[t][:, cols], axis=AXIS_X, op=ALU.max, apply_absolute_value=True)
-                    n_stats[0] += 1
-                    backlog.remove((c0, n, t))
-
-            PLAN = [("T", "w", 0), ("E", "w", 0), ("T", "b", 0), ("S", "x", 0), ("T", "x", 0), ("T", "w", 1), ("E", "x", 0), ("S", "x", 1), ("E", "b", 0), ("E", "w", 1), ("M", 0, 0), ("T", "x", 1), ("S", "x", 2), ("E", "x", 1), ("T", "x", 2), ("T", "w", 2), ("M", 1, 0), ("M", 0, 1), ("M", 1, 1), ("S", "x", 3), ("E", "x", 2), ("E", "w", 2), ("T", "x", 3), ("T", "w", 3), ("M", 0, 2), ("E", "x", 3), ("M", 1, 2), ("E", "w", 3), ("S", "x", 4), ("M", 0, 3), ("M", 1, 3), ("M", 2, 0), ("S", "x", 5), ("M", 3, 0), ("M", 2, 1), ("M", 3, 1), ("T", "x", 4), ("T", "x", 5), ("M", 2, 2), ("E", "x", 4), ("M", 3, 2), ("E", "x", 5), ("S", "x", 6), ("M", 2, 3), ("S", "x", 7), ("M", 3, 3), ("M", 0, 4), ("M", 1, 4), ("M", 2, 4), ("M", 3, 4), ("T", "x", 6), ("T", "x", 7), ("M", 0, 5), ("E", "x", 6), ("M", 1, 5), ("E", "x", 7), ("M", 2, 5), ("M", 3, 5), ("M", 0, 6), ("M", 1, 6), ("M", 2, 6), ("M", 3, 6), ("M", 0, 7), ("M", 1, 7), ("M", 2, 7), ("M", 3, 7)]
-            n_mult = len([op for op in PLAN if op[0] == "M"])
-            waiting = []
-            groups = []
-            pending = []
-            state = {"issued": 0, "retired": 0}
-
-            def some_pending(n):
-                for step in pending[state["issued"] : state["issued"] + n]:
-                    step()
-                state["issued"] = min(state["issued"] + n, len(pending))
-
-            def retire(keep_banks, flush):
-                while len(waiting) > keep_banks:
-                    c, t = waiting[0]
-                    waiting.remove((c, t))
-                    k = state["retired"]
-                    helped = 8 <= k <= 28 and k % 2 == 0
-                    add_bias(c, t, helped)
-                    state["retired"] = k + 1
-                    ready = k + 1 + (2 if helped else 0)
-                    g = groups[-1] if groups else None
-                    if g and g[2] == t and g[0] + g[1] == c and g[1] < 2 and k < n_mult - 2:
-                        groups[-1] = [g[0], g[1] + 1, t, max(g[3], ready)]
-                    else:
-                        groups.append([c, 1, t, ready])
-                    while groups and groups[0][3] <= state["retired"] and (len(groups) > 1 or groups[0][1] == 2 or k >= n_mult - 2):
-                        finish(groups[0][0], groups[0][1], groups[0][2])
-                        groups.remove(groups[0])
-                if flush:
-                    while groups:
-                        finish(groups[0][0], groups[0][1], groups[0][2])
-                        groups.remove(groups[0])
-
-            for op in PLAN:
-                if op[0] == "S":
-                    sort_x(op[2])
-                elif op[0] == "T":
-                    if op[1] == "b":
-                        spread_bias()
-                    else:
-                        transposes(op[1], op[2])
-                elif op[0] == "E":
-                    if op[1] == "b":
-                        copy_bias()
-                    else:
-                        empty(op[1], op[2])
-                        if op[1] == "w" and op[2] >= 2:
-                            pending.extend(quantize_steps(op[1], op[2]))
-                        else:
-                            for step in quantize_steps(op[1], op[2]):
-                                step()
-                else:
-                    multiply(op[1], op[2])
-                    waiting.append((op[1], op[2]))
-                    retire(1, False)
-                    some_pending(PEND_PER)
-                    if state["retired"] >= n_mult - 2 - 1:
-                        abs_max(len(backlog))
-                    elif state["retired"] >= 8:
-                        abs_max(1)
-            retire(0, True)
-            abs_max(len(backlog))
-
-        nc.vector.tensor_reduce(out=small[:, 2:3], in_=stats[:], axis=AXIS_X, op=ALU.max)
-        spread = psum.tile([P, P], F32, name="bank")
-        nc.tensor.transpose(spread[:], small[:, 2:3].to_broadcast([P, P]), ident_f[:])
-        nc.vector.tensor_reduce(out=small[:, 3:4], in_=spread[:], axis=AXIS_X, op=ALU.max)
+        nc.vector.tensor_reduce(out=small[:, 2:3], in_=maxima[:], axis=AXIS_X, op=ALU.max)
+        across = psum.tile([P, P], F32, name="bank")
+        nc.tensor.transpose(across[:], small[:, 2:3].to_broadcast([P, P]), identity[:])
+        nc.vector.tensor_reduce(out=small[:, 3:4], in_=across[:], axis=AXIS_X, op=ALU.max)
         inverse = small[:, 4:5]
         nc.vector.reciprocal(out=inverse, in_=small[:, 3:4])
 
         with ExitStack() as phase2:
-            ypool = phase2.enter_context(tc.tile_pool(name="ypool", bufs=3))
-            qpool = phase2.enter_context(tc.tile_pool(name="qpool", bufs=1))
+            scaled_pool = phase2.enter_context(tc.tile_pool(name="ypool", bufs=3))
+            bytes_pool = phase2.enter_context(tc.tile_pool(name="qpool", bufs=1))
             scaled = {}
 
             def scale(t):
-                yv = ypool.tile([P, V_COLS], F32, name="yv")
-                ys = ypool.tile([P, WIDTH - V_COLS], F32, name="ys")
-                nc.vector.tensor_scalar(out=yv[:], in0=o_sb[t][:, 0:V_COLS], scalar1=inverse, scalar2=448.0, op0=ALU.mult, op1=ALU.mult)
-                nc.scalar.activation(out=ys[:], in_=o_sb[t][:, V_COLS:WIDTH], func=ACT.Copy, scale=inverse)
-                scaled[t] = (yv, ys)
+                by_vector = scaled_pool.tile([P, V_COLS], F32, name="yv")
+                by_scalar = scaled_pool.tile([P, WIDTH - V_COLS], F32, name="ys")
+                nc.vector.tensor_scalar(out=by_vector[:], in0=result[t][:, 0:V_COLS], scalar1=inverse, scalar2=448.0, op0=ALU.mult, op1=ALU.mult)
+                nc.scalar.activation(out=by_scalar[:], in_=result[t][:, V_COLS:WIDTH], func=ACT.Copy, scale=inverse)
+                scaled[t] = (by_vector, by_scalar)
 
-            def cast(t):
-                yv, ys = scaled[t]
-                q8 = qpool.tile([P, WIDTH], FP8, name="q%d" % t)
-                nc.vector.tensor_copy(out=q8[:, 0:V_COLS], in_=yv[:], saturate=False)
-                nc.scalar.activation(out=q8[:, V_COLS:WIDTH], in_=ys[:], func=ACT.Copy, scale=448.0, saturate=False)
-                nc.sync.dma_start(out=o1[t * P : (t + 1) * P, :], in_=q8[:].bitcast(U8))
+            def cast_and_store(t):
+                by_vector, by_scalar = scaled[t]
+                codes = bytes_pool.tile([P, WIDTH], FP8, name="q%d" % t)
+                nc.vector.tensor_copy(out=codes[:, 0:V_COLS], in_=by_vector[:], saturate=False)
+                nc.scalar.activation(out=codes[:, V_COLS:WIDTH], in_=by_scalar[:], func=ACT.Copy, scale=448.0, saturate=False)
+                nc.sync.dma_start(out=byte_rows[t * P : (t + 1) * P, :], in_=codes[:].bitcast(U8))
 
             scale(0)
             for t in range(N_TILES):
                 if t + 1 < N_TILES:
                     scale(t + 1)
-                cast(t)
+                cast_and_store(t)

@@ -86,6 +86,7 @@ def tile_quaternionlinear_pa_kernel(tc, x, wr, wi, wj, wk, bias, out_0, out_1):
         bias_all = const.tile([P, WIDTH], BF16, name="bias_all")
         maxima = const.tile([P, N_BANKS], F32, name="maxima")
         small = const.tile([P, 8], F32, name="small")
+        zeros = const.tile([P, 1], F32, name="zeros")
 
         x_codes = [keep.tile([P, Q * P], U32, name="xc%d" % t, align_bytes=64) for t in range(N_TILES)]
         x_scales = [keep.tile([P, Q * P], U8, name="xs%d" % t, align_bytes=64) for t in range(N_TILES)]
@@ -104,6 +105,7 @@ def tile_quaternionlinear_pa_kernel(tc, x, wr, wi, wj, wk, bias, out_0, out_1):
             nc.vector.memset(bias_row[:], 0.0)
             nc.vector.memset(ones[:], 1.0)
             nc.vector.memset(small[:], 1.0)
+            nc.vector.memset(zeros[:], 0.0)
             nc.scalar.activation(out=small[:, 1:2], in_=small[:, 0:1], func=ACT.Copy)
             masks.make_identity(nc, identity[:])
 
@@ -361,28 +363,13 @@ def tile_quaternionlinear_pa_kernel(tc, x, wr, wi, wj, wk, bias, out_0, out_1):
         nc.vector.tensor_reduce(out=small[:, 3:4], in_=across[:], axis=AXIS_X, op=ALU.max)
         inverse = small[:, 4:5]
         nc.vector.reciprocal(out=inverse, in_=small[:, 3:4])
+        factor = small[:, 5:6]
+        nc.vector.tensor_scalar(out=factor, in0=inverse, scalar1=448.0, scalar2=None, op0=ALU.mult)
 
         with ExitStack() as phase2:
-            scaled_pool = phase2.enter_context(tc.tile_pool(name="ypool", bufs=3))
             bytes_pool = phase2.enter_context(tc.tile_pool(name="qpool", bufs=1))
-            scaled = {}
-
-            def scale(t):
-                by_vector = scaled_pool.tile([P, V_COLS], F32, name="yv")
-                by_scalar = scaled_pool.tile([P, WIDTH - V_COLS], F32, name="ys")
-                nc.vector.tensor_scalar(out=by_vector[:], in0=result[t][:, 0:V_COLS], scalar1=inverse, scalar2=448.0, op0=ALU.mult, op1=ALU.mult)
-                nc.scalar.activation(out=by_scalar[:], in_=result[t][:, V_COLS:WIDTH], func=ACT.Copy, scale=inverse)
-                scaled[t] = (by_vector, by_scalar)
-
-            def cast_and_store(t):
-                by_vector, by_scalar = scaled[t]
-                codes = bytes_pool.tile([P, WIDTH], FP8, name="q%d" % t)
-                nc.vector.tensor_copy(out=codes[:, 0:V_COLS], in_=by_vector[:], saturate=False)
-                nc.scalar.activation(out=codes[:, V_COLS:WIDTH], in_=by_scalar[:], func=ACT.Copy, scale=448.0, saturate=False)
-                nc.sync.dma_start(out=byte_rows[t * P : (t + 1) * P, :], in_=codes[:].bitcast(U8))
-
-            scale(0)
             for t in range(N_TILES):
-                if t + 1 < N_TILES:
-                    scale(t + 1)
-                cast_and_store(t)
+                codes = bytes_pool.tile([P, WIDTH], FP8, name="q%d" % t)
+                nc.vector.tensor_scalar(out=codes[:, 0:V_COLS], in0=result[t][:, 0:V_COLS], scalar1=factor, scalar2=None, op0=ALU.mult, saturate=False)
+                nc.scalar.activation(out=codes[:, V_COLS:WIDTH], in_=result[t][:, V_COLS:WIDTH], func=ACT.Identity, scale=factor, bias=zeros[:, 0:1], saturate=False)
+                nc.sync.dma_start(out=byte_rows[t * P : (t + 1) * P, :], in_=codes[:].bitcast(U8))

@@ -52,18 +52,23 @@ def helped(k):
     return HELPED_FIRST <= k <= HELPED_LAST and (k % 2 == 0 or k % 8 == 3)
 
 
-def quantize_runs():
-    flat = [block for row in MOVING for block in row]
+N_BLOCKS = 7
+QUANTIZE_RUNS = ((0, 4), (4, 2), (6, 1))
+
+
+def passes_of_a_bank():
     runs = []
-    d = 0
-    while d < len(flat):
-        n = 1
-        for longer in (4, 2):
-            if d + longer <= len(flat) and all(flat[d + e] == flat[d] + e for e in range(longer)):
-                n = longer
-                break
-        runs.append((flat[d], n, d))
-        d += n
+    for comp in range(Q):
+        row = MOVING[comp]
+        d = 0
+        while d < Q:
+            n = 1
+            for longer in (4, 2):
+                if d + longer <= Q and all(row[d + e] == row[d] + e for e in range(longer)):
+                    n = longer
+                    break
+            runs.append((comp, row[d], n, d))
+            d += n
     return runs
 
 
@@ -90,8 +95,8 @@ def tile_quaternionlinear_pa_kernel(tc, x, wr, wi, wj, wk, bias, out_0, out_1):
 
         x_codes = [keep.tile([P, Q * P], U32, name="xc%d" % t, align_bytes=64) for t in range(N_TILES)]
         x_scales = [keep.tile([P, Q * P], U8, name="xs%d" % t, align_bytes=64) for t in range(N_TILES)]
-        w_codes = [keep.tile([P, Q * BANK], U32, name="wc%d" % c, align_bytes=64) for c in range(N_CHUNKS)]
-        w_scales = [keep.tile([P, Q * BANK], U8, name="ws%d" % c, align_bytes=64) for c in range(N_CHUNKS)]
+        w_codes = [keep.tile([P, N_BLOCKS * P], U32, name="wc%d" % c, align_bytes=64) for c in range(N_CHUNKS)]
+        w_scales = [keep.tile([P, N_BLOCKS * P], U8, name="ws%d" % c, align_bytes=64) for c in range(N_CHUNKS)]
         result = [keep.tile([P, WIDTH], F32, name="o%d" % t) for t in range(N_TILES)]
 
         with ExitStack() as phase1:
@@ -199,14 +204,14 @@ def tile_quaternionlinear_pa_kernel(tc, x, wr, wi, wj, wk, bias, out_0, out_1):
                 plus = grouped[:, WI : WK + 1, :]
                 minus = grouped[:, NEG_WI : NEG_WK + 1, :]
 
-                def call(first, n, d):
+                def call(first, n):
                     return lambda: nc.vector.quantize_mx(
-                        out=w_codes[c][:, d * P : (d + n) * P].bitcast(FP8X4),
-                        scales=w_scales[c][:, d * P : (d + n) * P],
+                        out=w_codes[c][:, first * P : (first + n) * P].bitcast(FP8X4),
+                        scales=w_scales[c][:, first * P : (first + n) * P],
                         in_=grouped[:, first : first + n, :].rearrange("p b e -> p (b e)"),
                     )
 
-                calls = [call(first, n, d) for first, n, d in quantize_runs()]
+                calls = [call(first, n) for first, n in QUANTIZE_RUNS]
                 if c < 2:
                     nc.vector.tensor_scalar(out=minus, in0=plus, scalar1=-1.0, scalar2=None, op0=ALU.mult)
                     for one in calls:
@@ -271,15 +276,16 @@ def tile_quaternionlinear_pa_kernel(tc, x, wr, wi, wj, wk, bias, out_0, out_1):
 
             def bank(c, t):
                 sums = psum.tile([P, BANK], F32, name="bank")
-                for comp in range(Q):
+                runs = passes_of_a_bank()
+                for j, (comp, first, n, d) in enumerate(runs):
                     nc.tensor.matmul_mx(
-                        out=sums[:],
+                        out=sums[:, d * P : (d + n) * P],
                         lhsT=x_codes[t][:, comp * P : (comp + 1) * P].bitcast(FP8X4),
                         lhsT_scale=x_scales[t][:, comp * P : (comp + 1) * P],
-                        rhs=w_codes[c][:, comp * BANK : (comp + 1) * BANK].bitcast(FP8X4),
-                        rhs_scale=w_scales[c][:, comp * BANK : (comp + 1) * BANK],
-                        start=(comp == 0),
-                        stop=(comp == Q - 1),
+                        rhs=w_codes[c][:, first * P : (first + n) * P].bitcast(FP8X4),
+                        rhs_scale=w_scales[c][:, first * P : (first + n) * P],
+                        start=(j == 0),
+                        stop=(j == len(runs) - 1),
                     )
                 sums_of[(c, t)] = sums
                 multiplied.append((c, t))

@@ -39,21 +39,23 @@ MOVING = (
 )
 
 HELPED_FIRST = 8
-HELPED_LAST = 28
+HELPED_LAST = 30
 HELPED_LAG = 2
 QUANTIZE_CALLS_A_BANK = 6
 REDUCE_FROM = 8
 LAST_ALONE = 2
 
 V_COLS = 1376
+V_COLLECTS = 1
 
 
 def helped(k):
     return HELPED_FIRST <= k <= HELPED_LAST and (k % 2 == 0 or k % 8 == 3)
 
 
-N_BLOCKS = 7
-QUANTIZE_RUNS = ((0, 4), (4, 2), (6, 1))
+STRING = (NEG_WK, WR, WI, NEG_WI, WR, WJ, WK, NEG_WJ)
+N_BLOCKS = len(STRING)
+QUANTIZE_RUNS = ((0, 4), (4, 4))
 
 
 def passes_of_a_bank():
@@ -62,14 +64,15 @@ def passes_of_a_bank():
         row = MOVING[comp]
         d = 0
         while d < Q:
-            n = 1
-            for longer in (4, 2):
-                if d + longer <= Q and all(row[d + e] == row[d] + e for e in range(longer)):
-                    n = longer
-                    break
-            runs.append((comp, row[d], n, d))
-            d += n
-    return runs
+            pairs = [s for s in range(N_BLOCKS - 1) if d + 1 < Q and STRING[s] == row[d] and STRING[s + 1] == row[d + 1]]
+            if pairs:
+                runs.append((comp, pairs[0], 2, d))
+                d += 2
+            else:
+                runs.append((comp, STRING.index(row[d]), 1, d))
+                d += 1
+    early = [r for r in runs if r[1] + r[2] <= N_BLOCKS // 2]
+    return early + [r for r in runs if r not in early]
 
 
 def tile_quaternionlinear_pa_kernel(tc, x, wr, wi, wj, wk, bias, out_0, out_1):
@@ -175,10 +178,12 @@ def tile_quaternionlinear_pa_kernel(tc, x, wr, wi, wj, wk, bias, out_0, out_1):
             def collect_x(t):
                 grouped = stage.tile([P, Q, P, 4], BF16, name="xg", bufs=3, align_bytes=64)
                 for h in range(2):
-                    nc.scalar.copy(
-                        out=grouped[:, 2 * h : 2 * h + 2, :, :].rearrange("p c n t -> p c (n t)").bitcast(F32).rearrange("p c (n u) -> p c n u", u=2),
-                        in_=turned[("x", t)][h][:].rearrange("p (c u) n -> p c n u", c=2),
-                    )
+                    target = grouped[:, 2 * h : 2 * h + 2, :, :].rearrange("p c n t -> p c (n t)").bitcast(F32).rearrange("p c (n u) -> p c n u", u=2)
+                    source = turned[("x", t)][h][:].rearrange("p (c u) n -> p c n u", c=2)
+                    if t < V_COLLECTS and h == 1:
+                        nc.vector.tensor_copy(out=target, in_=source)
+                    else:
+                        nc.scalar.copy(out=target, in_=source)
                 nc.vector.quantize_mx(out=x_codes[t][:].bitcast(FP8X4), scales=x_scales[t][:], in_=grouped[:].rearrange("p c n t -> p (c n t)"))
 
             later_calls = []
@@ -195,14 +200,14 @@ def tile_quaternionlinear_pa_kernel(tc, x, wr, wi, wj, wk, bias, out_0, out_1):
                 turned[("w", c)] = banks
 
             def collect_w(c):
-                grouped = stage.tile([P, 7, IQ], BF16, name="wg", bufs=2, align_bytes=64)
-                for h in range(2):
-                    nc.scalar.copy(
-                        out=grouped[:, 2 * h : 2 * h + 2, :].bitcast(F32).rearrange("p y (o u) -> p y o u", u=2),
-                        in_=turned[("w", c)][h][:].rearrange("p y u o -> p y o u"),
-                    )
-                plus = grouped[:, WI : WK + 1, :]
-                minus = grouped[:, NEG_WI : NEG_WK + 1, :]
+                grouped = stage.tile([P, N_BLOCKS, IQ], BF16, name="wg", bufs=2, align_bytes=64)
+                for target, source in (
+                    (grouped[:, 1:3, :], turned[("w", c)][0][:]),
+                    (grouped[:, 5:7, :], turned[("w", c)][1][:]),
+                    (grouped[:, 4:5, :], turned[("w", c)][0][:, 0:1, :, :]),
+                ):
+                    nc.scalar.copy(out=target.bitcast(F32).rearrange("p y (o u) -> p y o u", u=2), in_=source.rearrange("p y u o -> p y o u"))
+                negations = ((grouped[:, 3:8:4, :], grouped[:, 2:6:3, :]), (grouped[:, 0:1, :], grouped[:, 6:7, :]))
 
                 def call(first, n):
                     return lambda: nc.vector.quantize_mx(
@@ -213,11 +218,13 @@ def tile_quaternionlinear_pa_kernel(tc, x, wr, wi, wj, wk, bias, out_0, out_1):
 
                 calls = [call(first, n) for first, n in QUANTIZE_RUNS]
                 if c < 2:
-                    nc.vector.tensor_scalar(out=minus, in0=plus, scalar1=-1.0, scalar2=None, op0=ALU.mult)
+                    for minus, plus in negations:
+                        nc.vector.tensor_scalar(out=minus, in0=plus, scalar1=-1.0, scalar2=None, op0=ALU.mult)
                     for one in calls:
                         one()
                 else:
-                    nc.scalar.activation(out=minus, in_=plus, func=ACT.Copy, scale=-1.0)
+                    for minus, plus in negations:
+                        nc.scalar.activation(out=minus, in_=plus, func=ACT.Copy, scale=-1.0)
                     later_calls.extend(calls)
 
             sums_of = {}

@@ -46,6 +46,8 @@ REDUCE_FROM = 8
 LAST_ALONE = 2
 
 V_COLS = 1376
+V_CHUNKS = 1
+S_SORTS_FROM = 4
 V_COLLECTS = 1
 
 
@@ -158,7 +160,7 @@ def tile_quaternionlinear_pa_kernel(tc, x, wr, wi, wj, wk, bias, out_0, out_1):
                 source = x_raw[t][:].rearrange("r (p u e c) -> r c u p e", u=2, e=2, c=Q)
                 for c in range(Q):
                     target = tile[:, c, :].rearrange("r (u p e) -> r u p e", u=2, e=2)
-                    if c < 2:
+                    if c < 2 or t >= S_SORTS_FROM:
                         nc.scalar.copy(out=target, in_=source[:, c])
                     else:
                         nc.gpsimd.tensor_scalar(out=target, in0=source[:, c], scalar1=1.0, scalar2=0.0, op0=ALU.mult, op1=ALU.add)
@@ -206,7 +208,10 @@ def tile_quaternionlinear_pa_kernel(tc, x, wr, wi, wj, wk, bias, out_0, out_1):
                     (grouped[:, 5:7, :], turned[("w", c)][1][:]),
                     (grouped[:, 4:5, :], turned[("w", c)][0][:, 0:1, :, :]),
                 ):
-                    nc.scalar.copy(out=target.bitcast(F32).rearrange("p y (o u) -> p y o u", u=2), in_=source.rearrange("p y u o -> p y o u"))
+                    if c < V_CHUNKS:
+                        nc.vector.tensor_copy(out=target.bitcast(F32).rearrange("p y (o u) -> p y o u", u=2), in_=source.rearrange("p y u o -> p y o u"))
+                    else:
+                        nc.scalar.copy(out=target.bitcast(F32).rearrange("p y (o u) -> p y o u", u=2), in_=source.rearrange("p y u o -> p y o u"))
                 negations = ((grouped[:, 3:8:4, :], grouped[:, 2:6:3, :]), (grouped[:, 0:1, :], grouped[:, 6:7, :]))
 
                 def call(first, n):

@@ -96,6 +96,7 @@ def tile_quaternionlinear_pa_kernel(tc, x, wr, wi, wj, wk, bias, out_0, out_1):
         bias_all = const.tile([P, WIDTH], BF16, name="bias_all")
         maxima = const.tile([P, N_BANKS], F32, name="maxima")
         small = const.tile([P, 8], F32, name="small")
+        scaled_maxima = const.tile([P, N_BANKS], F32, name="scaled_maxima")
         zeros = const.tile([P, 1], F32, name="zeros")
 
         x_codes = [keep.tile([P, Q * P], U32, name="xc%d" % t, align_bytes=64) for t in range(N_TILES)]
@@ -375,14 +376,12 @@ def tile_quaternionlinear_pa_kernel(tc, x, wr, wi, wj, wk, bias, out_0, out_1):
             store_ready_runs(True)
             reduce_oldest(len(unreduced))
 
-        nc.vector.tensor_reduce(out=small[:, 2:3], in_=maxima[:], axis=AXIS_X, op=ALU.max)
+        nc.vector.tensor_scalar(out=scaled_maxima[:], in0=maxima[:], scalar1=1.0 / 448.0, scalar2=None, op0=ALU.mult, op1=ALU.max, accum_out=small[:, 2:3])
         across = psum.tile([P, P], F32, name="bank")
         nc.tensor.transpose(across[:], small[:, 2:3].to_broadcast([P, P]), identity[:])
         nc.vector.tensor_reduce(out=small[:, 3:4], in_=across[:], axis=AXIS_X, op=ALU.max)
-        inverse = small[:, 4:5]
-        nc.vector.reciprocal(out=inverse, in_=small[:, 3:4])
-        factor = small[:, 5:6]
-        nc.vector.tensor_scalar(out=factor, in0=inverse, scalar1=448.0, scalar2=None, op0=ALU.mult)
+        factor = small[:, 4:5]
+        nc.vector.reciprocal(out=factor, in_=small[:, 3:4])
 
         with ExitStack() as phase2:
             bytes_pool = phase2.enter_context(tc.tile_pool(name="qpool", bufs=1))

@@ -94,16 +94,16 @@ def tile_quaternionlinear_pa_kernel(tc, x, wr, wi, wj, wk, bias, out_0, out_1):
         ones = const.tile([P, P], BF16, name="ones")
         bias_row = const.tile([P, WIDTH], BF16, name="bias_row")
         bias_all = const.tile([P, WIDTH], BF16, name="bias_all")
-        maxima = const.tile([P, N_BANKS], F32, name="maxima")
         small = const.tile([P, 8], F32, name="small")
-        scaled_maxima = const.tile([P, N_BANKS], F32, name="scaled_maxima")
+        scaled = const.tile([P, P], F32, name="scaled")
         zeros = const.tile([P, 1], F32, name="zeros")
 
         x_codes = [keep.tile([P, Q * P], U32, name="xc%d" % t, align_bytes=64) for t in range(N_TILES)]
         x_scales = [keep.tile([P, Q * P], U8, name="xs%d" % t, align_bytes=64) for t in range(N_TILES)]
         w_codes = [keep.tile([P, N_BLOCKS * P], U32, name="wc%d" % c, align_bytes=64) for c in range(N_CHUNKS)]
         w_scales = [keep.tile([P, N_BLOCKS * P], U8, name="ws%d" % c, align_bytes=64) for c in range(N_CHUNKS)]
-        result = [keep.tile([P, WIDTH], F32, name="o%d" % t) for t in range(N_TILES)]
+        result = [keep.tile([P, WIDTH + (N_BANKS if t == N_TILES - 1 else 0)], F32, name="o%d" % t) for t in range(N_TILES)]
+        maxima = result[N_TILES - 1][:, WIDTH : WIDTH + N_BANKS]
 
         with ExitStack() as phase1:
             raw = phase1.enter_context(tc.tile_pool(name="raw", bufs=1))
@@ -112,7 +112,7 @@ def tile_quaternionlinear_pa_kernel(tc, x, wr, wi, wj, wk, bias, out_0, out_1):
             x_raw = [raw.tile([P, WIDTH], BF16, name="xr%d" % t) for t in range(N_TILES)]
             w_raw = [raw.tile([P, Q, IQ], BF16, name="wr%d" % c) for c in range(N_CHUNKS)]
 
-            nc.vector.memset(maxima[:], 0.0)
+            nc.vector.memset(maxima, 0.0)
             nc.vector.memset(bias_row[:], 0.0)
             nc.vector.memset(ones[:], 1.0)
             nc.vector.memset(small[:], 1.0)
@@ -207,7 +207,6 @@ def tile_quaternionlinear_pa_kernel(tc, x, wr, wi, wj, wk, bias, out_0, out_1):
                 for target, source in (
                     (grouped[:, 1:3, :], turned[("w", c)][0][:]),
                     (grouped[:, 5:7, :], turned[("w", c)][1][:]),
-                    (grouped[:, 4:5, :], turned[("w", c)][0][:, 0:1, :, :]),
                 ):
                     if c < V_CHUNKS:
                         nc.vector.tensor_copy(out=target.bitcast(F32).rearrange("p y (o u) -> p y o u", u=2), in_=source.rearrange("p y u o -> p y o u"))
@@ -222,15 +221,16 @@ def tile_quaternionlinear_pa_kernel(tc, x, wr, wi, wj, wk, bias, out_0, out_1):
                         in_=grouped[:, first : first + n, :].rearrange("p b e -> p (b e)"),
                     )
 
-                calls = [call(first, n) for first, n in QUANTIZE_RUNS]
-                if c < 2:
+                def complete():
+                    nc.vector.tensor_copy(out=grouped[:, 4:5, :], in_=grouped[:, 1:2, :])
                     for minus, plus in negations:
                         nc.vector.tensor_scalar(out=minus, in0=plus, scalar1=-1.0, scalar2=None, op0=ALU.mult)
+
+                calls = [complete] + [call(first, n) for first, n in QUANTIZE_RUNS]
+                if c < 2:
                     for one in calls:
                         one()
                 else:
-                    for minus, plus in negations:
-                        nc.scalar.activation(out=minus, in_=plus, func=ACT.Copy, scale=-1.0)
                     later_calls.extend(calls)
 
             sums_of = {}
@@ -278,9 +278,10 @@ def tile_quaternionlinear_pa_kernel(tc, x, wr, wi, wj, wk, bias, out_0, out_1):
             def reduce_oldest(n):
                 for c0, chunks, t in unreduced[:n]:
                     unreduced.remove((c0, chunks, t))
+                    last = t == N_TILES - 1 and c0 + chunks == N_CHUNKS
                     nc.vector.tensor_reduce(
-                        out=maxima[:, count["maxima"] : count["maxima"] + 1],
-                        in_=result[t][:, c0 * BANK : (c0 + chunks) * BANK],
+                        out=small[:, 2:3] if last else maxima[:, count["maxima"] : count["maxima"] + 1],
+                        in_=result[t][:, c0 * BANK : WIDTH + N_BANKS if last else (c0 + chunks) * BANK],
                         axis=AXIS_X,
                         op=ALU.max,
                         apply_absolute_value=True,
@@ -376,10 +377,9 @@ def tile_quaternionlinear_pa_kernel(tc, x, wr, wi, wj, wk, bias, out_0, out_1):
             store_ready_runs(True)
             reduce_oldest(len(unreduced))
 
-        nc.vector.tensor_scalar(out=scaled_maxima[:], in0=maxima[:], scalar1=1.0 / 448.0, scalar2=None, op0=ALU.mult, op1=ALU.max, accum_out=small[:, 2:3])
         across = psum.tile([P, P], F32, name="bank")
         nc.tensor.transpose(across[:], small[:, 2:3].to_broadcast([P, P]), identity[:])
-        nc.vector.tensor_reduce(out=small[:, 3:4], in_=across[:], axis=AXIS_X, op=ALU.max)
+        nc.vector.tensor_scalar(out=scaled[:], in0=across[:], scalar1=1.0 / 448.0, scalar2=None, op0=ALU.mult, op1=ALU.max, accum_out=small[:, 3:4])
         factor = small[:, 4:5]
         nc.vector.reciprocal(out=factor, in_=small[:, 3:4])
 

@@ -191,14 +191,21 @@ def tile_quaternionlinear_pa_kernel(tc, x, wr, wi, wj, wk, bias, out_0, out_1):
 
             later_calls = []
 
+            sorted_w = {}
+
+            def sort_w(c):
+                tile = stage.tile([P, Q, IQ], BF16, name="ws", bufs=1)
+                nc.scalar.copy(out=tile[:].bitcast(F32).rearrange("p y (u k) -> p y u k", u=2), in_=w_raw[c][:].bitcast(F32).rearrange("p y (k u) -> p y u k", u=2))
+                sorted_w[c] = tile
+
             def transpose_w(c):
                 banks = []
                 for h in range(2):
                     bank = psum.tile([P, 2, 2, P], F32, name="bank")
                     for yy in range(2):
-                        words = w_raw[c][:, 2 * h + yy, :].bitcast(F32)
+                        words = (sorted_w[c] if c in sorted_w else w_raw[c])[:, 2 * h + yy, :].bitcast(F32)
                         for u in range(2):
-                            nc.tensor.transpose(bank[:, yy, u, :], words[:, u::2], identity[:])
+                            nc.tensor.transpose(bank[:, yy, u, :], words[:, u * P : (u + 1) * P] if c in sorted_w else words[:, u::2], identity[:])
                     banks.append(bank)
                 turned[("w", c)] = banks
 
@@ -316,10 +323,10 @@ def tile_quaternionlinear_pa_kernel(tc, x, wr, wi, wj, wk, bias, out_0, out_1):
 
             transpose_w(0)
             collect_w(0)
-            spread_bias()
             sort_x(0)
             transpose_x(0)
             transpose_w(1)
+            spread_bias()
             collect_x(0)
             sort_x(1)
             copy_bias()
@@ -336,6 +343,7 @@ def tile_quaternionlinear_pa_kernel(tc, x, wr, wi, wj, wk, bias, out_0, out_1):
             sort_x(3)
             collect_x(2)
             collect_w(2)
+            sort_w(3)
             transpose_x(3)
             transpose_w(3)
             bank(0, 2)
@@ -387,6 +395,10 @@ def tile_quaternionlinear_pa_kernel(tc, x, wr, wi, wj, wk, bias, out_0, out_1):
             bytes_pool = phase2.enter_context(tc.tile_pool(name="qpool", bufs=1))
             for t in range(N_TILES):
                 codes = bytes_pool.tile([P, WIDTH], FP8, name="q%d" % t)
-                nc.vector.tensor_scalar(out=codes[:, 0:V_COLS], in0=result[t][:, 0:V_COLS], scalar1=factor, scalar2=None, op0=ALU.mult, saturate=False)
-                nc.scalar.activation(out=codes[:, V_COLS:WIDTH], in_=result[t][:, V_COLS:WIDTH], func=ACT.Identity, scale=factor, bias=zeros[:, 0:1], saturate=False)
-                nc.sync.dma_start(out=byte_rows[t * P : (t + 1) * P, :], in_=codes[:].bitcast(U8))
+                pieces = 2 if t == N_TILES - 1 else 1
+                for first in range(0, WIDTH, WIDTH // pieces):
+                    mid = first + V_COLS // pieces
+                    end = first + WIDTH // pieces
+                    nc.vector.tensor_scalar(out=codes[:, first:mid], in0=result[t][:, first:mid], scalar1=factor, scalar2=None, op0=ALU.mult, saturate=False)
+                    nc.scalar.activation(out=codes[:, mid:end], in_=result[t][:, mid:end], func=ACT.Identity, scale=factor, bias=zeros[:, 0:1], saturate=False)
+                    nc.sync.dma_start(out=byte_rows[t * P : (t + 1) * P, first:end], in_=codes[:, first:end].bitcast(U8))

from contextlib import ExitStack

import concourse.masks as masks
import concourse.mybir as mybir

FLOPS = 2 * 10 * 1024 * 512 * 512

F32 = mybir.dt.float32
BF16 = mybir.dt.bfloat16
U32 = mybir.dt.uint32
U8 = mybir.dt.uint8
FP8 = mybir.dt.float8_e4m3fn
FP8X4 = mybir.dt.float8_e4m3fn_x4
ALU = mybir.AluOpType
ACT = mybir.ActivationFunctionType
AXIS_X = mybir.AxisListType.X

P = 128
Q = 4
IQ = 512
N_TILES = 8
N_CHUNKS = 4
BANK = Q * P
WIDTH = N_CHUNKS * BANK
N_BANKS = N_CHUNKS * N_TILES

WR = 0
WI = 1
WJ = 2
WK = 3
NEG_WI = 4
NEG_WJ = 5
NEG_WK = 6
MOVING = (
    (WR, WI, WJ, WK),
    (NEG_WI, WR, WI, NEG_WI),
    (NEG_WJ, NEG_WJ, WR, WJ),
    (NEG_WK, WK, NEG_WK, WR),
)

HELPED_FIRST = 8
HELPED_LAST = 30
HELPED_LAG = 2
QUANTIZE_CALLS_A_BANK = 6
REDUCE_FROM = 8
LAST_ALONE = 2

V_COLS = 1376
V_CHUNKS = 1
S_SORTS_FROM = 4
V_COLLECTS = 1


def helped(k):
    return HELPED_FIRST <= k <= HELPED_LAST and (k % 2 == 0 or k % 8 == 3)


STRING = (NEG_WK, WR, WI, NEG_WI, WR, WJ, WK, NEG_WJ)
N_BLOCKS = len(STRING)
QUANTIZE_RUNS = ((0, 4), (4, 4))


def passes_of_a_bank():
    runs = []
    for comp in range(Q):
        row = MOVING[comp]
        d = 0
        while d < Q:
            pairs = [s for s in range(N_BLOCKS - 1) if d + 1 < Q and STRING[s] == row[d] and STRING[s + 1] == row[d + 1]]
            if pairs:
                runs.append((comp, pairs[0], 2, d))
                d += 2
            else:
                runs.append((comp, STRING.index(row[d]), 1, d))
                d += 1
    early = [r for r in runs if r[1] + r[2] <= N_BLOCKS // 2]
    return early + [r for r in runs if r not in early]


def tile_quaternionlinear_pa_kernel(tc, x, wr, wi, wj, wk, bias, out_0, out_1):
    nc = tc.nc
    x_rows = x.flatten_outer_dims()
    out_rows = out_0.flatten_outer_dims()
    byte_rows = out_1.flatten_outer_dims()
    weights = (wr, wi, wj, wk)

    with ExitStack() as ctx:
        const = ctx.enter_context(tc.tile_pool(name="const", bufs=1))
        keep = ctx.enter_context(tc.tile_pool(name="keep", bufs=1))
        psum = ctx.enter_context(tc.psum_pool(name="psum", bufs=8))
        ctx.enter_context(tc.manual_schedule())

        identity = const.tile([P, P], F32, name="identity")
        ones = const.tile([P, P], BF16, name="ones")
        bias_row = const.tile([P, WIDTH], BF16, name="bias_row")
        bias_all = const.tile([P, WIDTH], BF16, name="bias_all")
        small = const.tile([P, 8], F32, name="small")
        scaled = const.tile([P, P], F32, name="scaled")
        zeros = const.tile([P, 1], F32, name="zeros")

        x_codes = [keep.tile([P, Q * P], U32, name="xc%d" % t, align_bytes=64) for t in range(N_TILES)]
        x_scales = [keep.tile([P, Q * P], U8, name="xs%d" % t, align_bytes=64) for t in range(N_TILES)]
        w_codes = [keep.tile([P, N_BLOCKS * P], U32, name="wc%d" % c, align_bytes=64) for c in range(N_CHUNKS)]
        w_scales = [keep.tile([P, N_BLOCKS * P], U8, name="ws%d" % c, align_bytes=64) for c in range(N_CHUNKS)]
        result = [keep.tile([P, WIDTH + (N_BANKS if t == N_TILES - 1 else 0)], F32, name="o%d" % t) for t in range(N_TILES)]
        maxima = result[N_TILES - 1][:, WIDTH : WIDTH + N_BANKS]

        with ExitStack() as phase1:
            raw = phase1.enter_context(tc.tile_pool(name="raw", bufs=1))
            stage = phase1.enter_context(tc.tile_pool(name="stage", bufs=3))

            x_raw = [raw.tile([P, WIDTH], BF16, name="xr%d" % t) for t in range(N_TILES)]
            w_raw = [raw.tile([P, Q, IQ], BF16, name="wr%d" % c) for c in range(N_CHUNKS)]

            nc.vector.memset(maxima, 0.0)
            nc.vector.memset(bias_row[:], 0.0)
            nc.vector.memset(ones[:], 1.0)
            nc.vector.memset(small[:], 1.0)
            nc.vector.memset(zeros[:], 0.0)
            nc.scalar.activation(out=small[:, 1:2], in_=small[:, 0:1], func=ACT.Copy)
            masks.make_identity(nc, identity[:])

            def load_w(c):
                for y in range(Q):
                    nc.sync.dma_start(out=w_raw[c][:, y, :], in_=weights[y][c * P : (c + 1) * P, :])

            def load_x(t):
                nc.sync.dma_start(out=x_raw[t][:], in_=x_rows[t * P : (t + 1) * P, :])

            load_w(0)
            load_x(0)
            nc.sync.dma_start(out=bias_row[0:1, :], in_=bias.rearrange("(a n) -> a n", a=1))
            load_w(1)
            load_x(1)
            load_x(2)
            load_w(2)
            load_x(3)
            load_w(3)
            for t in range(4, N_TILES):
                load_x(t)

            bias_banks = []

            def spread_bias():
                for h in range(2):
                    spread = psum.tile([P, 2 * BANK], BF16, name="bank")
                    for e in range(2):
                        cols = slice((2 * h + e) * BANK, (2 * h + e + 1) * BANK)
                        nc.tensor.matmul(out=spread[:, e * BANK : (e + 1) * BANK], lhsT=ones[:], rhs=bias_row[:, cols], start=True, stop=True)
                    bias_banks.append(spread)

            def copy_bias():
                for h in range(2):
                    nc.vector.tensor_copy(out=bias_all[:, 2 * h * BANK : 2 * (h + 1) * BANK], in_=bias_banks[h][:])

            sorted_x = {}
            turned = {}

            def sort_x(t):
                tile = stage.tile([P, Q, IQ], BF16, name="xs", bufs=3)
                source = x_raw[t][:].rearrange("r (p u e c) -> r c u p e", u=2, e=2, c=Q)
                for c in range(Q):
                    target = tile[:, c, :].rearrange("r (u p e) -> r u p e", u=2, e=2)
                    if c < 2 or t >= S_SORTS_FROM:
                        nc.scalar.copy(out=target, in_=source[:, c])
                    else:
                        nc.gpsimd.tensor_scalar(out=target, in0=source[:, c], scalar1=1.0, scalar2=0.0, op0=ALU.mult, op1=ALU.add)
                sorted_x[t] = tile

            def transpose_x(t):
                banks = []
                for h in range(2):
                    bank = psum.tile([P, 4, P], F32, name="bank")
                    for cc in range(2):
                        words = sorted_x[t][:, 2 * h + cc, :].bitcast(F32)
                        for u in range(2):
                            nc.tensor.transpose(bank[:, cc * 2 + u, :], words[:, u * P : (u + 1) * P], identity[:])
                    banks.append(bank)
                turned[("x", t)] = banks

            def collect_x(t):
                grouped = stage.tile([P, Q, P, 4], BF16, name="xg", bufs=3, align_bytes=64)
                for h in range(2):
                    target = grouped[:, 2 * h : 2 * h + 2, :, :].rearrange("p c n t -> p c (n t)").bitcast(F32).rearrange("p c (n u) -> p c n u", u=2)
                    source = turned[("x", t)][h][:].rearrange("p (c u) n -> p c n u", c=2)
                    if t < V_COLLECTS and h == 1:
                        nc.vector.tensor_copy(out=target, in_=source)
                    else:
                        nc.scalar.copy(out=target, in_=source)
                nc.vector.quantize_mx(out=x_codes[t][:].bitcast(FP8X4), scales=x_scales[t][:], in_=grouped[:].rearrange("p c n t -> p (c n t)"))

            later_calls = []

            sorted_w = {}

            def sort_w(c):
                tile = stage.tile([P, Q, IQ], BF16, name="ws", bufs=1)
                nc.scalar.copy(out=tile[:].bitcast(F32).rearrange("p y (u k) -> p y u k", u=2), in_=w_raw[c][:].bitcast(F32).rearrange("p y (k u) -> p y u k", u=2))
                sorted_w[c] = tile

            def transpose_w(c):
                banks = []
                for h in range(2):
                    bank = psum.tile([P, 2, 2, P], F32, name="bank")
                    for yy in range(2):
                        words = (sorted_w[c] if c in sorted_w else w_raw[c])[:, 2 * h + yy, :].bitcast(F32)
                        for u in range(2):
                            nc.tensor.transpose(bank[:, yy, u, :], words[:, u * P : (u + 1) * P] if c in sorted_w else words[:, u::2], identity[:])
                    banks.append(bank)
                turned[("w", c)] = banks

            def collect_w(c):
                grouped = stage.tile([P, N_BLOCKS, IQ], BF16, name="wg", bufs=2, align_bytes=64)
                for target, source in (
                    (grouped[:, 1:3, :], turned[("w", c)][0][:]),
                    (grouped[:, 5:7, :], turned[("w", c)][1][:]),
                ):
                    if c < V_CHUNKS:
                        nc.vector.tensor_copy(out=target.bitcast(F32).rearrange("p y (o u) -> p y o u", u=2), in_=source.rearrange("p y u o -> p y o u"))
                    else:
                        nc.scalar.copy(out=target.bitcast(F32).rearrange("p y (o u) -> p y o u", u=2), in_=source.rearrange("p y u o -> p y o u"))
                negations = ((grouped[:, 3:8:4, :], grouped[:, 2:6:3, :]), (grouped[:, 0:1, :], grouped[:, 6:7, :]))

                def call(first, n):
                    return lambda: nc.vector.quantize_mx(
                        out=w_codes[c][:, first * P : (first + n) * P].bitcast(FP8X4),
                        scales=w_scales[c][:, first * P : (first + n) * P],
                        in_=grouped[:, first : first + n, :].rearrange("p b e -> p (b e)"),
                    )

                def complete():
                    nc.vector.tensor_copy(out=grouped[:, 4:5, :], in_=grouped[:, 1:2, :])
                    for minus, plus in negations:
                        nc.vector.tensor_scalar(out=minus, in0=plus, scalar1=-1.0, scalar2=None, op0=ALU.mult)

                calls = [complete] + [call(first, n) for first, n in QUANTIZE_RUNS]
                if c < 2:
                    for one in calls:
                        one()
                else:
                    later_calls.extend(calls)

            sums_of = {}
            multiplied = []
            open_runs = []
            unreduced = []
            count = {"biased": 0, "calls": 0, "maxima": 0}

            def add_bias(c, t, k):
                cols = slice(c * BANK, (c + 1) * BANK)
                sums = sums_of[(c, t)][:].rearrange("p (c o) -> p o c", c=Q)
                if helped(k):
                    plain = stage.tile([P, BANK], F32, name="plain", bufs=3)
                    nc.scalar.copy(out=plain[:].rearrange("p (o c) -> p o c", c=Q), in_=sums)
                    nc.gpsimd.tensor_tensor(out=result[t][:, cols], in0=plain[:], in1=bias_all[:, cols], op=ALU.add)
                else:
                    nc.vector.tensor_tensor(
                        out=result[t][:, cols].rearrange("p (o c) -> p o c", c=Q),
                        in0=sums,
                        in1=bias_all[:, cols].rearrange("p (o c) -> p o c", c=Q),
                        op=ALU.add,
                    )

            def store_ready_runs(everything):
                while open_runs and (everything or (open_runs[0][3] <= count["biased"] and (len(open_runs) > 1 or open_runs[0][1] == 2 or count["biased"] > N_BANKS - LAST_ALONE))):
                    c0, n, t = open_runs[0][:3]
                    open_runs.remove(open_runs[0])
                    cols = slice(c0 * BANK, (c0 + n) * BANK)
                    nc.sync.dma_start(out=out_rows[t * P : (t + 1) * P, cols], in_=result[t][:, cols])
                    unreduced.append((c0, n, t))

            def retire_oldest():
                c, t = multiplied[0]
                multiplied.remove((c, t))
                k = count["biased"]
                add_bias(c, t, k)
                count["biased"] = k + 1
                ready = k + 1 + (HELPED_LAG if helped(k) else 0)
                last = open_runs[-1] if open_runs else None
                if last and last[2] == t and last[0] + last[1] == c and last[1] < 2 and k < N_BANKS - LAST_ALONE:
                    open_runs[-1] = [last[0], 2, t, max(last[3], ready)]
                else:
                    open_runs.append([c, 1, t, ready])

            def reduce_oldest(n):
                for c0, chunks, t in unreduced[:n]:
                    unreduced.remove((c0, chunks, t))
                    last = t == N_TILES - 1 and c0 + chunks == N_CHUNKS
                    nc.vector.tensor_reduce(
                        out=small[:, 2:3] if last else maxima[:, count["maxima"] : count["maxima"] + 1],
                        in_=result[t][:, c0 * BANK : WIDTH + N_BANKS if last else (c0 + chunks) * BANK],
                        axis=AXIS_X,
                        op=ALU.max,
                        apply_absolute_value=True,
                    )
                    count["maxima"] += 1

            def bank(c, t):
                sums = psum.tile([P, BANK], F32, name="bank")
                runs = passes_of_a_bank()
                for j, (comp, first, n, d) in enumerate(runs):
                    nc.tensor.matmul_mx(
                        out=sums[:, d * P : (d + n) * P],
                        lhsT=x_codes[t][:, comp * P : (comp + 1) * P].bitcast(FP8X4),
                        lhsT_scale=x_scales[t][:, comp * P : (comp + 1) * P],
                        rhs=w_codes[c][:, first * P : (first + n) * P].bitcast(FP8X4),
                        rhs_scale=w_scales[c][:, first * P : (first + n) * P],
                        start=(j == 0),
                        stop=(j == len(runs) - 1),
                    )
                sums_of[(c, t)] = sums
                multiplied.append((c, t))
                if len(multiplied) > 1:
                    retire_oldest()
                    store_ready_runs(False)
                for one in later_calls[count["calls"] : count["calls"] + QUANTIZE_CALLS_A_BANK]:
                    one()
                count["calls"] = min(count["calls"] + QUANTIZE_CALLS_A_BANK, len(later_calls))
                if count["biased"] >= N_BANKS - LAST_ALONE - 1:
                    reduce_oldest(len(unreduced))
                elif count["biased"] >= REDUCE_FROM:
                    reduce_oldest(1)

            transpose_w(0)
            collect_w(0)
            sort_x(0)
            transpose_x(0)
            transpose_w(1)
            spread_bias()
            collect_x(0)
            sort_x(1)
            copy_bias()
            collect_w(1)
            bank(0, 0)
            transpose_x(1)
            sort_x(2)
            collect_x(1)
            transpose_x(2)
            transpose_w(2)
            bank(1, 0)
            bank(0, 1)
            bank(1, 1)
            sort_x(3)
            collect_x(2)
            collect_w(2)
            sort_w(3)
            transpose_x(3)
            transpose_w(3)
            bank(0, 2)
            collect_x(3)
            bank(1, 2)
            collect_w(3)
            sort_x(4)
            bank(0, 3)
            bank(1, 3)
            bank(2, 0)
            sort_x(5)
            bank(3, 0)
            bank(2, 1)
            bank(3, 1)
            transpose_x(4)
            transpose_x(5)
            bank(2, 2)
            collect_x(4)
            bank(3, 2)
            collect_x(5)
            sort_x(6)
            bank(2, 3)
            sort_x(7)
            bank(3, 3)
            for c in range(N_CHUNKS):
                bank(c, 4)
            transpose_x(6)
            transpose_x(7)
            bank(0, 5)
            collect_x(6)
            bank(1, 5)
            collect_x(7)
            bank(2, 5)
            bank(3, 5)
            for t in (6, 7):
                for c in range(N_CHUNKS):
                    bank(c, t)
            retire_oldest()
            store_ready_runs(True)
            reduce_oldest(len(unreduced))

        across = psum.tile([P, P], F32, name="bank")
        nc.tensor.transpose(across[:], small[:, 2:3].to_broadcast([P, P]), identity[:])
        nc.vector.tensor_scalar(out=scaled[:], in0=across[:], scalar1=1.0 / 448.0, scalar2=None, op0=ALU.mult, op1=ALU.max, accum_out=small[:, 3:4])
        factor = small[:, 4:5]
        nc.vector.reciprocal(out=factor, in_=small[:, 3:4])

        with ExitStack() as phase2:
            bytes_pool = phase2.enter_context(tc.tile_pool(name="qpool", bufs=1))
            for t in range(N_TILES):
                codes = bytes_pool.tile([P, WIDTH], FP8, name="q%d" % t)
                pieces = 2 if t == N_TILES - 1 else 1
                for first in range(0, WIDTH, WIDTH // pieces):
                    mid = first + V_COLS // pieces
                    end = first + WIDTH // pieces
                    nc.vector.tensor_scalar(out=codes[:, first:mid], in0=result[t][:, first:mid], scalar1=factor, scalar2=None, op0=ALU.mult, saturate=False)
                    nc.scalar.activation(out=codes[:, mid:end], in_=result[t][:, mid:end], func=ACT.Identity, scale=factor, bias=zeros[:, 0:1], saturate=False)
                    nc.sync.dma_start(out=byte_rows[t * P : (t + 1) * P, first:end], in_=codes[:, first:end].bitcast(U8))
